import numpy as np
import ml_dtypes


def mxq(x, axis, fmt="e4m3"):
    dtype, down = {"e4m3": (ml_dtypes.float8_e4m3fn, 7), "e5m2": (ml_dtypes.float8_e5m2, 14)}[fmt]
    v = np.moveaxis(np.asarray(x, np.float32).astype(ml_dtypes.bfloat16).astype(np.float64), axis, -1)
    blocks = v.reshape(v.shape[:-1] + (-1, 32))
    amax = np.abs(blocks).max(-1, keepdims=True)
    byte = np.maximum(np.where(amax > 0, np.frexp(amax)[1] - 1 + 127, 0) - down, 1)
    scale = np.exp2(byte - 127.0)
    codes = (blocks / scale).astype(np.float32).astype(dtype).astype(np.float64)
    return np.moveaxis((codes * scale).reshape(v.shape), -1, axis)


WIDE = False


def mx_kscale(k):
    if not WIDE:
        return np.ones(k)
    levels = np.array([10, -10, 5, -5, 0])
    a = np.random.permutation(np.resize(levels, k // 512 * 4)).reshape(k // 512, 4)
    idx = np.arange(k)
    return np.exp2(a[idx // 512, idx % 128 // 32])


BF16 = ml_dtypes.bfloat16


def bf(x):
    return np.asarray(x, np.float32).astype(BF16)


def f64(x):
    return np.asarray(x).astype(np.float64)


N, H, S, R, T = 512, 16384, 4, 128, 128


def setup_inputs():
    s = mx_kscale(H)
    return {"encodings": bf(np.random.standard_normal((N, H)) * s),
            "domain_encs": bf(np.random.standard_normal((S, H)) * s),
            "Us": bf(np.random.standard_normal((S, H, R)) / np.sqrt(H) / s[None, :, None])}


def reference(encodings, domain_encs, Us):
    diff = f64(encodings)[None, :, :] - f64(domain_encs)[:, None, :]
    proj = mxq(diff, 2, "e4m3") @ mxq(f64(Us), 1, "e4m3")
    dist = np.sqrt(np.sum(proj * proj, axis=-1))
    z = -dist
    e = np.exp(z - z.max(axis=0, keepdims=True))
    return e / e.sum(axis=0, keepdims=True)

@@ -1,0 +1,201 @@
+from contextlib import ExitStack
+
+import concourse.mybir as mybir
+from concourse.masks import make_identity
+
+F32 = mybir.dt.float32
+BF16 = mybir.dt.bfloat16
+U32 = mybir.dt.uint32
+U8 = mybir.dt.uint8
+FP8X4 = mybir.dt.float8_e4m3fn_x4
+ACT = mybir.ActivationFunctionType
+ALU = mybir.AluOpType
+AXIS = mybir.AxisListType
+
+P = 128
+PACK = 4
+K_PASS = P * PACK
+PAIR = 2
+
+TOKENS = 512
+HIDDEN = 16384
+SOURCES = 4
+RANK = 128
+PASSES = HIDDEN // K_PASS
+TOKEN_BLOCKS = TOKENS // P
+BANK_WORDS = 512
+BANK_TOKENS = BANK_WORDS // PAIR
+BANKS_PER_PASS = TOKENS // BANK_TOKENS
+PASSES_PER_LOAD = 2
+LOAD_K = PASSES_PER_LOAD * K_PASS
+QUANT_COLS = 4096
+SOURCES_PER_QUANT = QUANT_COLS // (TOKENS * PACK)
+ONES_COLS = 2
+
+FLOPS = 2 * SOURCES * TOKENS * HIDDEN * RANK
+
+
+def tile_moe_pa_k_kernel(tc, encodings, domain_encs, Us, out):
+    nc = tc.nc
+    with ExitStack() as ctx:
+        const = ctx.enter_context(tc.tile_pool(name="const", bufs=1))
+        loads = ctx.enter_context(tc.tile_pool(name="loads", bufs=3))
+        work = ctx.enter_context(tc.tile_pool(name="work", bufs=3))
+        acc_pool = ctx.enter_context(tc.psum_pool(name="acc", bufs=1))
+        bank_pool = ctx.enter_context(tc.psum_pool(name="banks", bufs=4))
+
+        ident = const.tile([P, P], F32)
+        make_identity(nc, ident[:])
+
+        warm = const.tile([P, 1], F32)
+        nc.vector.memset(warm[:], 1.0)
+        nc.scalar.activation(out=warm[:], in_=warm[:], func=ACT.Sqrt)
+
+        d_rows = const.tile([P, K_PASS], BF16)
+        nc.sync.dma_start(out=d_rows[:], in_=domain_encs.rearrange("s (g k) -> (s g) k", k=K_PASS))
+        d_words = d_rows[:].bitcast(F32).rearrange("r (w u) -> r u w", u=PAIR)
+        d_bank = bank_pool.tile([P, BANK_WORDS], F32, tag="bank")
+        for u in range(PAIR):
+            nc.tensor.transpose(d_bank[:, u * P : (u + 1) * P], d_words[:, u, :], ident[:])
+        d_cols = const.tile([P, SOURCES * PASSES * PACK], BF16)
+        nc.vector.tensor_copy(
+            out=d_cols[:].bitcast(F32).rearrange("p (r u) -> p r u", u=PAIR),
+            in_=d_bank[:, 0 : PAIR * P].rearrange("p (u r) -> p r u", u=PAIR),
+        )
+
+        acc = [acc_pool.tile([P, TOKENS], F32, name="acc%d" % s) for s in range(SOURCES)]
+
+        for load in range(PASSES // PASSES_PER_LOAD):
+            k_lo = load * LOAD_K
+            x_sb = loads.tile([P, TOKEN_BLOCKS, LOAD_K], BF16)
+            nc.sync.dma_start(
+                out=x_sb[:],
+                in_=encodings[:, k_lo : k_lo + LOAD_K].rearrange("(b n) k -> n b k", n=P),
+            )
+            u_raw = loads.tile([P, SOURCES, PASSES_PER_LOAD, PACK * RANK], BF16)
+            for s in range(SOURCES):
+                nc.sync.dma_start(
+                    out=u_raw[:, s],
+                    in_=Us[s, k_lo : k_lo + LOAD_K, :].rearrange("(g p t) r -> p g (t r)", p=P, t=PACK),
+                )
+
+            for g_in_load in range(PASSES_PER_LOAD):
+                g = load * PASSES_PER_LOAD + g_in_load
+
+                u_grouped = work.tile([P, SOURCES, RANK, PACK], BF16, align_bytes=64)
+                for s in range(SOURCES):
+                    nc.scalar.copy(
+                        out=u_grouped[:, s].rearrange("p (c i) t -> p c t i", i=4),
+                        in_=u_raw[:, s, g_in_load].rearrange("p (t c i) -> p c t i", t=PACK, i=4),
+                    )
+                u_codes = work.tile([P, SOURCES * RANK], U32, align_bytes=64)
+                u_scales = work.tile([P, SOURCES * RANK], U8, align_bytes=64)
+
+                banks = []
+                for half in range(BANKS_PER_PASS):
+                    bank = bank_pool.tile([P, BANK_WORDS], F32, tag="bank")
+                    for b_in_bank in range(BANK_TOKENS // P):
+                        b = half * (BANK_TOKENS // P) + b_in_bank
+                        x_words = (
+                            x_sb[:, b, g_in_load * K_PASS : (g_in_load + 1) * K_PASS]
+                            .bitcast(F32)
+                            .rearrange("n (w u) -> n u w", u=PAIR)
+                        )
+                        for u in range(PAIR):
+                            col = u * BANK_TOKENS + b_in_bank * P
+                            nc.tensor.transpose(bank[:, col : col + P], x_words[:, u, :], ident[:])
+                    banks.append(bank)
+
+                diff = work.tile([P, SOURCES, TOKENS, PACK], BF16, align_bytes=64)
+                for half in range(BANKS_PER_PASS):
+                    for s in range(SOURCES):
+                        d_col = (s * PASSES + g) * PACK
+                        nc.vector.tensor_tensor(
+                            out=diff[:, s, half * BANK_TOKENS : (half + 1) * BANK_TOKENS, :].rearrange(
+                                "p n (u e) -> p n u e", e=PAIR
+                            ),
+                            in0=banks[half][:].bitcast(BF16).rearrange("p (u n e) -> p n u e", u=PAIR, e=PAIR),
+                            in1=d_cols[:, d_col : d_col + PACK]
+                            .rearrange("p (u e) -> p u e", e=PAIR)
+                            .unsqueeze(1)
+                            .to_broadcast([P, BANK_TOKENS, PAIR, PAIR]),
+                            op=ALU.subtract,
+                        )
+
+                nc.vector.quantize_mx(
+                    out=u_codes[:].bitcast(FP8X4),
+                    scales=u_scales[:],
+                    in_=u_grouped[:].rearrange("p s r t -> p (s r t)"),
+                )
+                diff_codes = work.tile([P, SOURCES, TOKENS], U32, align_bytes=64)
+                diff_scales = work.tile([P, SOURCES, TOKENS], U8, align_bytes=64)
+                for s_lo in range(0, SOURCES, SOURCES_PER_QUANT):
+                    s_hi = s_lo + SOURCES_PER_QUANT
+                    nc.vector.quantize_mx(
+                        out=diff_codes[:, s_lo:s_hi, :].rearrange("p s n -> p (s n)").bitcast(FP8X4),
+                        scales=diff_scales[:, s_lo:s_hi, :].rearrange("p s n -> p (s n)"),
+                        in_=diff[:, s_lo:s_hi].rearrange("p s n t -> p (s n t)"),
+                    )
+
+                for s in range(SOURCES):
+                    nc.tensor.matmul_mx(
+                        out=acc[s][:],
+                        lhsT=u_codes[:, s * RANK : (s + 1) * RANK].bitcast(FP8X4),
+                        lhsT_scale=u_scales[:, s * RANK : (s + 1) * RANK],
+                        rhs=diff_codes[:, s, :].bitcast(FP8X4),
+                        rhs_scale=diff_scales[:, s, :],
+                        start=(g == 0),
+                        stop=(g == PASSES - 1),
+                    )
+
+        ones = const.tile([P, ONES_COLS], F32)
+        nc.vector.memset(ones[:], 1.0)
+        dist2 = bank_pool.tile([P, BANK_WORDS], F32, tag="bank")
+        n_cols = SOURCES * TOKEN_BLOCKS
+        for s in range(SOURCES):
+            squares = const.tile([P, TOKENS], F32, name="squares%d" % s)
+            nc.scalar.activation(out=squares[:], in_=acc[s][:], func=ACT.Square)
+            for b in range(TOKEN_BLOCKS):
+                col = (s * TOKEN_BLOCKS + b) * ONES_COLS
+                nc.tensor.matmul(
+                    out=dist2[:, col : col + ONES_COLS],
+                    lhsT=squares[:, b * P : (b + 1) * P],
+                    rhs=ones[:],
+                    start=True,
+                    stop=True,
+                )
+
+        dist = const.tile([P, SOURCES, TOKEN_BLOCKS], F32)
+        nc.scalar.activation(
+            out=dist[:].rearrange("p s b -> p (s b)"),
+            in_=dist2[:, 0 : n_cols * ONES_COLS].rearrange("p (c o) -> p c o", o=ONES_COLS)[:, :, 0],
+            func=ACT.Sqrt,
+        )
+        nearest = const.tile([P, TOKEN_BLOCKS], F32)
+        nc.vector.tensor_reduce(out=nearest[:], in_=dist[:].rearrange("p s b -> p b s"), axis=AXIS.X, op=ALU.min)
+        excess = const.tile([P, SOURCES, TOKEN_BLOCKS], F32)
+        nc.vector.tensor_tensor(
+            out=excess[:],
+            in0=dist[:],
+            in1=nearest[:].unsqueeze(1).to_broadcast([P, SOURCES, TOKEN_BLOCKS]),
+            op=ALU.subtract,
+        )
+        weights = const.tile([P, SOURCES, TOKEN_BLOCKS], F32)
+        nc.scalar.activation(out=weights[:], in_=excess[:], func=ACT.Exp, scale=-1.0)
+        total = const.tile([P, TOKEN_BLOCKS], F32)
+        nc.vector.tensor_reduce(out=total[:], in_=weights[:].rearrange("p s b -> p b s"), axis=AXIS.X, op=ALU.add)
+        inv_total = const.tile([P, TOKEN_BLOCKS], F32)
+        nc.vector.reciprocal(out=inv_total[:], in_=total[:])
+        alphas = const.tile([P, P], F32)
+        nc.vector.memset(alphas[:], 0.0)
+        nc.vector.tensor_tensor(
+            out=alphas[:, 0:n_cols].rearrange("p (s b) -> p s b", s=SOURCES),
+            in0=weights[:],
+            in1=inv_total[:].unsqueeze(1).to_broadcast([P, SOURCES, TOKEN_BLOCKS]),
+            op=ALU.mult,
+        )
+        alphas_bank = bank_pool.tile([P, BANK_WORDS], F32, tag="bank")
+        nc.tensor.transpose(alphas_bank[:, 0:P], alphas[:], ident[:])
+        alphas_rows = const.tile([P, P], F32)
+        nc.vector.tensor_copy(out=alphas_rows[:], in_=alphas_bank[:, 0:P])
+        nc.sync.dma_start(out=out.rearrange("s (b n) -> (s b) n", n=P), in_=alphas_rows[0:n_cols, :])

@@ -20,16 +20,18 @@ PAIR = 2
 TOKENS = 512
 HIDDEN = 16384
 SOURCES = 4
+LAST = SOURCES - 1
 RANK = 128
 PASSES = HIDDEN // K_PASS
 TOKEN_BLOCKS = TOKENS // P
 BANK_WORDS = 512
 BANK_TOKENS = BANK_WORDS // PAIR
 BANKS_PER_PASS = TOKENS // BANK_TOKENS
+BLOCKS_PER_BANK = BANK_TOKENS // P
 PASSES_PER_LOAD = 2
+LOADS = PASSES // PASSES_PER_LOAD
+LOADS_AHEAD = 2
 LOAD_K = PASSES_PER_LOAD * K_PASS
-QUANT_COLS = 4096
-SOURCES_PER_QUANT = QUANT_COLS // (TOKENS * PACK)
 ONES_COLS = 2
 
 FLOPS = 2 * SOURCES * TOKENS * HIDDEN * RANK
@@ -39,34 +41,24 @@ def tile_moe_pa_k_kernel(tc, encodings, domain_encs, Us, out):
     nc = tc.nc
     with ExitStack() as ctx:
         const = ctx.enter_context(tc.tile_pool(name="const", bufs=1))
-        loads = ctx.enter_context(tc.tile_pool(name="loads", bufs=3))
-        work = ctx.enter_context(tc.tile_pool(name="work", bufs=3))
+        loads = ctx.enter_context(tc.tile_pool(name="loads", bufs=LOADS_AHEAD + 1))
+        work = ctx.enter_context(tc.tile_pool(name="work", bufs=2))
+        single = ctx.enter_context(tc.tile_pool(name="single", bufs=1))
         acc_pool = ctx.enter_context(tc.psum_pool(name="acc", bufs=1))
-        bank_pool = ctx.enter_context(tc.psum_pool(name="banks", bufs=4))
+        bank_pool = ctx.enter_context(tc.psum_pool(name="banks", bufs=2 * BANKS_PER_PASS))
+        ctx.enter_context(tc.manual_schedule())
 
-        ident = const.tile([P, P], F32)
-        make_identity(nc, ident[:])
+        x_of_load = {}
+        u_of_load = {}
+        banks_of_pass = {}
+        planes_of_pass = {}
+        u_grouped_of_pass = {}
+        diff_of_pass = {}
+        diff_last_of_pass = {}
+        codes_of_pass = {}
 
-        warm = const.tile([P, 1], F32)
-        nc.vector.memset(warm[:], 1.0)
-        nc.scalar.activation(out=warm[:], in_=warm[:], func=ACT.Sqrt)
-
-        d_rows = const.tile([P, K_PASS], BF16)
-        nc.sync.dma_start(out=d_rows[:], in_=domain_encs.rearrange("s (g k) -> (s g) k", k=K_PASS))
-        d_words = d_rows[:].bitcast(F32).rearrange("r (w u) -> r u w", u=PAIR)
-        d_bank = bank_pool.tile([P, BANK_WORDS], F32, tag="bank")
-        for u in range(PAIR):
-            nc.tensor.transpose(d_bank[:, u * P : (u + 1) * P], d_words[:, u, :], ident[:])
-        d_cols = const.tile([P, SOURCES * PASSES * PACK], BF16)
-        nc.vector.tensor_copy(
-            out=d_cols[:].bitcast(F32).rearrange("p (r u) -> p r u", u=PAIR),
-            in_=d_bank[:, 0 : PAIR * P].rearrange("p (u r) -> p r u", u=PAIR),
-        )
-
-        acc = [acc_pool.tile([P, TOKENS], F32, name="acc%d" % s) for s in range(SOURCES)]
-
-        for load in range(PASSES // PASSES_PER_LOAD):
-            k_lo = load * LOAD_K
+        def load(round_):
+            k_lo = round_ * LOAD_K
             x_sb = loads.tile([P, TOKEN_BLOCKS, LOAD_K], BF16)
             nc.sync.dma_start(
                 out=x_sb[:],
@@ -78,78 +70,164 @@ def tile_moe_pa_k_kernel(tc, encodings, domain_encs, Us, out):
                     out=u_raw[:, s],
                     in_=Us[s, k_lo : k_lo + LOAD_K, :].rearrange("(g p t) r -> p g (t r)", p=P, t=PACK),
                 )
+            x_of_load[round_] = x_sb
+            u_of_load[round_] = u_raw
 
-            for g_in_load in range(PASSES_PER_LOAD):
-                g = load * PASSES_PER_LOAD + g_in_load
-
-                u_grouped = work.tile([P, SOURCES, RANK, PACK], BF16, align_bytes=64)
-                for s in range(SOURCES):
-                    nc.scalar.copy(
-                        out=u_grouped[:, s].rearrange("p (c i) t -> p c t i", i=4),
-                        in_=u_raw[:, s, g_in_load].rearrange("p (t c i) -> p c t i", t=PACK, i=4),
+        def transpose_pass(g):
+            x_sb = x_of_load[g // PASSES_PER_LOAD]
+            k_lo = (g % PASSES_PER_LOAD) * K_PASS
+            banks = []
+            for half in range(BANKS_PER_PASS):
+                bank = bank_pool.tile([P, BANK_WORDS], F32, tag="bank")
+                for b_in_bank in range(BLOCKS_PER_BANK):
+                    x_words = (
+                        x_sb[:, half * BLOCKS_PER_BANK + b_in_bank, k_lo : k_lo + K_PASS]
+                        .bitcast(F32)
+                        .rearrange("n (w u) -> n u w", u=PAIR)
                     )
-                u_codes = work.tile([P, SOURCES * RANK], U32, align_bytes=64)
-                u_scales = work.tile([P, SOURCES * RANK], U8, align_bytes=64)
+                    for u in range(PAIR):
+                        col = u * BANK_TOKENS + b_in_bank * P
+                        nc.tensor.transpose(bank[:, col : col + P], x_words[:, u, :], ident[:])
+                banks.append(bank)
+            banks_of_pass[g] = banks
 
-                banks = []
-                for half in range(BANKS_PER_PASS):
-                    bank = bank_pool.tile([P, BANK_WORDS], F32, tag="bank")
-                    for b_in_bank in range(BANK_TOKENS // P):
-                        b = half * (BANK_TOKENS // P) + b_in_bank
-                        x_words = (
-                            x_sb[:, b, g_in_load * K_PASS : (g_in_load + 1) * K_PASS]
-                            .bitcast(F32)
-                            .rearrange("n (w u) -> n u w", u=PAIR)
-                        )
-                        for u in range(PAIR):
-                            col = u * BANK_TOKENS + b_in_bank * P
-                            nc.tensor.transpose(bank[:, col : col + P], x_words[:, u, :], ident[:])
-                    banks.append(bank)
+        def bank_values(bank):
+            return bank[:].bitcast(BF16).rearrange("p (u n e) -> p n u e", u=PAIR, e=PAIR)
 
-                diff = work.tile([P, SOURCES, TOKENS, PACK], BF16, align_bytes=64)
-                for half in range(BANKS_PER_PASS):
-                    for s in range(SOURCES):
-                        d_col = (s * PASSES + g) * PACK
-                        nc.vector.tensor_tensor(
-                            out=diff[:, s, half * BANK_TOKENS : (half + 1) * BANK_TOKENS, :].rearrange(
-                                "p n (u e) -> p n u e", e=PAIR
-                            ),
-                            in0=banks[half][:].bitcast(BF16).rearrange("p (u n e) -> p n u e", u=PAIR, e=PAIR),
-                            in1=d_cols[:, d_col : d_col + PACK]
-                            .rearrange("p (u e) -> p u e", e=PAIR)
-                            .unsqueeze(1)
-                            .to_broadcast([P, BANK_TOKENS, PAIR, PAIR]),
-                            op=ALU.subtract,
-                        )
-
-                nc.vector.quantize_mx(
-                    out=u_codes[:].bitcast(FP8X4),
-                    scales=u_scales[:],
-                    in_=u_grouped[:].rearrange("p s r t -> p (s r t)"),
+        def scalar_pass(g):
+            planes = work.tile([P, PACK, TOKENS], BF16)
+            for half in range(BANKS_PER_PASS):
+                for t in range(PACK):
+                    nc.scalar.activation(
+                        out=planes[:, t, half * BANK_TOKENS : (half + 1) * BANK_TOKENS],
+                        in_=bank_values(banks_of_pass[g][half])[:, :, t // PAIR, t % PAIR],
+                        func=ACT.Identity,
+                        bias=neg_d_last[:, g * PACK + t : g * PACK + t + 1],
+                        scale=1.0,
+                    )
+            planes_of_pass[g] = planes
+            u_raw = u_of_load[g // PASSES_PER_LOAD]
+            u_grouped = work.tile([P, SOURCES, RANK, PACK], BF16, align_bytes=64)
+            for s in range(SOURCES):
+                nc.scalar.copy(
+                    out=u_grouped[:, s].rearrange("p (c i) t -> p c t i", i=4),
+                    in_=u_raw[:, s, g % PASSES_PER_LOAD].rearrange("p (t c i) -> p c t i", t=PACK, i=4),
                 )
-                diff_codes = work.tile([P, SOURCES, TOKENS], U32, align_bytes=64)
-                diff_scales = work.tile([P, SOURCES, TOKENS], U8, align_bytes=64)
-                for s_lo in range(0, SOURCES, SOURCES_PER_QUANT):
-                    s_hi = s_lo + SOURCES_PER_QUANT
-                    nc.vector.quantize_mx(
-                        out=diff_codes[:, s_lo:s_hi, :].rearrange("p s n -> p (s n)").bitcast(FP8X4),
-                        scales=diff_scales[:, s_lo:s_hi, :].rearrange("p s n -> p (s n)"),
-                        in_=diff[:, s_lo:s_hi].rearrange("p s n t -> p (s n t)"),
-                    )
+            u_grouped_of_pass[g] = u_grouped
 
-                for s in range(SOURCES):
-                    nc.tensor.matmul_mx(
-                        out=acc[s][:],
-                        lhsT=u_codes[:, s * RANK : (s + 1) * RANK].bitcast(FP8X4),
-                        lhsT_scale=u_scales[:, s * RANK : (s + 1) * RANK],
-                        rhs=diff_codes[:, s, :].bitcast(FP8X4),
-                        rhs_scale=diff_scales[:, s, :],
-                        start=(g == 0),
-                        stop=(g == PASSES - 1),
-                    )
+        def interleave_last(g):
+            diff_last = single.tile([P, TOKENS, PACK], BF16, align_bytes=64)
+            nc.gpsimd.tensor_scalar(
+                out=diff_last[:],
+                in0=planes_of_pass[g][:].rearrange("p t n -> p n t"),
+                scalar1=1.0,
+                scalar2=0.0,
+                op0=ALU.mult,
+                op1=ALU.add,
+            )
+            diff_last_of_pass[g] = diff_last
 
+        def subtract_pass(g):
+            diff = work.tile([P, LAST, TOKENS, PACK], BF16, align_bytes=64)
+            for half in range(BANKS_PER_PASS):
+                for s in range(LAST):
+                    d_col = (s * PASSES + g) * PACK
+                    nc.vector.tensor_tensor(
+                        out=diff[:, s, half * BANK_TOKENS : (half + 1) * BANK_TOKENS, :].rearrange(
+                            "p n (u e) -> p n u e", e=PAIR
+                        ),
+                        in0=bank_values(banks_of_pass[g][half]),
+                        in1=d_cols[:, d_col : d_col + PACK]
+                        .rearrange("p (u e) -> p u e", e=PAIR)
+                        .unsqueeze(1)
+                        .to_broadcast([P, BANK_TOKENS, PAIR, PAIR]),
+                        op=ALU.subtract,
+                    )
+            diff_of_pass[g] = diff
+
+        def quantise_pass(g):
+            u_codes = work.tile([P, SOURCES * RANK], U32, align_bytes=64)
+            u_scales = work.tile([P, SOURCES * RANK], U8, align_bytes=64)
+            nc.vector.quantize_mx(
+                out=u_codes[:].bitcast(FP8X4),
+                scales=u_scales[:],
+                in_=u_grouped_of_pass[g][:].rearrange("p s r t -> p (s r t)"),
+            )
+            diff_codes = work.tile([P, SOURCES, TOKENS], U32, align_bytes=64)
+            diff_scales = work.tile([P, SOURCES, TOKENS], U8, align_bytes=64)
+            for s in range(SOURCES):
+                values = diff_of_pass[g][:, s] if s < LAST else diff_last_of_pass[g][:]
+                nc.vector.quantize_mx(
+                    out=diff_codes[:, s, :].bitcast(FP8X4),
+                    scales=diff_scales[:, s, :],
+                    in_=values.rearrange("p n t -> p (n t)"),
+                )
+            codes_of_pass[g] = (u_codes, u_scales, diff_codes, diff_scales)
+
+        def multiply_pass(g):
+            u_codes, u_scales, diff_codes, diff_scales = codes_of_pass[g]
+            for s in range(SOURCES):
+                nc.tensor.matmul_mx(
+                    out=acc[s][:],
+                    lhsT=u_codes[:, s * RANK : (s + 1) * RANK].bitcast(FP8X4),
+                    lhsT_scale=u_scales[:, s * RANK : (s + 1) * RANK],
+                    rhs=diff_codes[:, s, :].bitcast(FP8X4),
+                    rhs_scale=diff_scales[:, s, :],
+                    start=(g == 0),
+                    stop=(g == PASSES - 1),
+                )
+
+        d_rows = const.tile([P, K_PASS], BF16)
+        nc.sync.dma_start(out=d_rows[:], in_=domain_encs.rearrange("s (g k) -> (s g) k", k=K_PASS))
+        for round_ in range(LOADS_AHEAD):
+            load(round_)
+
+        ident = const.tile([P, P], F32)
+        make_identity(nc, ident[:])
         ones = const.tile([P, ONES_COLS], F32)
         nc.vector.memset(ones[:], 1.0)
+        alphas = const.tile([P, P], F32)
+        nc.vector.memset(alphas[:], 0.0)
+        warm = const.tile([P, 1], F32)
+        nc.vector.memset(warm[:], 1.0)
+        nc.scalar.activation(out=warm[:], in_=warm[:], func=ACT.Sqrt)
+
+        d_words = d_rows[:].bitcast(F32).rearrange("r (w u) -> r u w", u=PAIR)
+        d_bank = bank_pool.tile([P, BANK_WORDS], F32, tag="bank")
+        for u in range(PAIR):
+            nc.tensor.transpose(d_bank[:, u * P : (u + 1) * P], d_words[:, u, :], ident[:])
+        d_cols = const.tile([P, SOURCES * PASSES * PACK], BF16)
+        nc.vector.tensor_copy(
+            out=d_cols[:].bitcast(F32).rearrange("p (r u) -> p r u", u=PAIR),
+            in_=d_bank[:, 0 : PAIR * P].rearrange("p (u r) -> p r u", u=PAIR),
+        )
+        neg_d_last = const.tile([P, PASSES * PACK], F32)
+        nc.vector.tensor_scalar(
+            out=neg_d_last[:],
+            in0=d_cols[:, LAST * PASSES * PACK : SOURCES * PASSES * PACK],
+            scalar1=-1.0,
+            scalar2=None,
+            op0=ALU.mult,
+        )
+
+        acc = [acc_pool.tile([P, TOKENS], F32, name="acc%d" % s) for s in range(SOURCES)]
+
+        transpose_pass(0)
+        transpose_pass(1)
+        scalar_pass(0)
+        for g in range(PASSES):
+            round_ = g // PASSES_PER_LOAD + LOADS_AHEAD
+            if g % PASSES_PER_LOAD == 0 and round_ < LOADS:
+                load(round_)
+            interleave_last(g)
+            subtract_pass(g)
+            if g + 2 < PASSES:
+                transpose_pass(g + 2)
+            if g + 1 < PASSES:
+                scalar_pass(g + 1)
+            quantise_pass(g)
+            multiply_pass(g)
+
         dist2 = bank_pool.tile([P, BANK_WORDS], F32, tag="bank")
         n_cols = SOURCES * TOKEN_BLOCKS
         for s in range(SOURCES):
@@ -186,8 +264,6 @@ def tile_moe_pa_k_kernel(tc, encodings, domain_encs, Us, out):
         nc.vector.tensor_reduce(out=total[:], in_=weights[:].rearrange("p s b -> p b s"), axis=AXIS.X, op=ALU.add)
         inv_total = const.tile([P, TOKEN_BLOCKS], F32)
         nc.vector.reciprocal(out=inv_total[:], in_=total[:])
-        alphas = const.tile([P, P], F32)
-        nc.vector.memset(alphas[:], 0.0)
         nc.vector.tensor_tensor(
             out=alphas[:, 0:n_cols].rearrange("p (s b) -> p s b", s=SOURCES),
             in0=weights[:],

@@ -28,10 +28,10 @@ BANK_WORDS = 512
 BANK_TOKENS = BANK_WORDS // PAIR
 BANKS_PER_PASS = TOKENS // BANK_TOKENS
 BLOCKS_PER_BANK = BANK_TOKENS // P
-PASSES_PER_LOAD = 2
-LOADS = PASSES // PASSES_PER_LOAD
-LOADS_AHEAD = 2
-LOAD_K = PASSES_PER_LOAD * K_PASS
+TRANSPOSE_LAG = 2
+SCALAR_LAG = 3
+SUBTRACT_LAG = 4
+MULTIPLY_LAG = 5
 ONES_COLS = 2
 
 FLOPS = 2 * SOURCES * TOKENS * HIDDEN * RANK
@@ -41,15 +41,15 @@ def tile_moe_pa_k_kernel(tc, encodings, domain_encs, Us, out):
     nc = tc.nc
     with ExitStack() as ctx:
         const = ctx.enter_context(tc.tile_pool(name="const", bufs=1))
-        loads = ctx.enter_context(tc.tile_pool(name="loads", bufs=LOADS_AHEAD + 1))
+        loads = ctx.enter_context(tc.tile_pool(name="loads", bufs=SCALAR_LAG + 1))
         work = ctx.enter_context(tc.tile_pool(name="work", bufs=2))
-        single = ctx.enter_context(tc.tile_pool(name="single", bufs=1))
+        ahead = ctx.enter_context(tc.tile_pool(name="ahead", bufs=MULTIPLY_LAG - SCALAR_LAG + 1))
         acc_pool = ctx.enter_context(tc.psum_pool(name="acc", bufs=1))
         bank_pool = ctx.enter_context(tc.psum_pool(name="banks", bufs=2 * BANKS_PER_PASS))
         ctx.enter_context(tc.manual_schedule())
 
-        x_of_load = {}
-        u_of_load = {}
+        x_of_pass = {}
+        u_of_pass = {}
         banks_of_pass = {}
         planes_of_pass = {}
         u_grouped_of_pass = {}
@@ -57,66 +57,75 @@ def tile_moe_pa_k_kernel(tc, encodings, domain_encs, Us, out):
         diff_last_of_pass = {}
         codes_of_pass = {}
 
-        def load(round_):
-            k_lo = round_ * LOAD_K
-            x_sb = loads.tile([P, TOKEN_BLOCKS, LOAD_K], BF16)
+        def is_pass(g):
+            return 0 <= g < PASSES
+
+        def load(g):
+            if not is_pass(g):
+                return
+            k_lo = g * K_PASS
+            x_sb = loads.tile([P, TOKEN_BLOCKS, K_PASS], BF16)
             nc.sync.dma_start(
                 out=x_sb[:],
-                in_=encodings[:, k_lo : k_lo + LOAD_K].rearrange("(b n) k -> n b k", n=P),
+                in_=encodings[:, k_lo : k_lo + K_PASS].rearrange("(b n) k -> n b k", n=P),
             )
-            u_raw = loads.tile([P, SOURCES, PASSES_PER_LOAD, PACK * RANK], BF16)
-            for s in range(SOURCES):
-                nc.sync.dma_start(
-                    out=u_raw[:, s],
-                    in_=Us[s, k_lo : k_lo + LOAD_K, :].rearrange("(g p t) r -> p g (t r)", p=P, t=PACK),
-                )
-            x_of_load[round_] = x_sb
-            u_of_load[round_] = u_raw
+            u_raw = loads.tile([P, SOURCES, PACK * RANK], BF16)
+            nc.sync.dma_start(
+                out=u_raw[:],
+                in_=Us[:, k_lo : k_lo + K_PASS, :].rearrange("s (p t) r -> p s (t r)", t=PACK),
+            )
+            x_of_pass[g] = x_sb
+            u_of_pass[g] = u_raw
 
         def transpose_pass(g):
-            x_sb = x_of_load[g // PASSES_PER_LOAD]
-            k_lo = (g % PASSES_PER_LOAD) * K_PASS
+            if not is_pass(g):
+                return
             banks = []
             for half in range(BANKS_PER_PASS):
                 bank = bank_pool.tile([P, BANK_WORDS], F32, tag="bank")
+                bank_words = bank[:].rearrange("p (n u) -> p u n", u=PAIR)
                 for b_in_bank in range(BLOCKS_PER_BANK):
                     x_words = (
-                        x_sb[:, half * BLOCKS_PER_BANK + b_in_bank, k_lo : k_lo + K_PASS]
+                        x_of_pass[g][:, half * BLOCKS_PER_BANK + b_in_bank, :]
                         .bitcast(F32)
                         .rearrange("n (w u) -> n u w", u=PAIR)
                     )
                     for u in range(PAIR):
-                        col = u * BANK_TOKENS + b_in_bank * P
-                        nc.tensor.transpose(bank[:, col : col + P], x_words[:, u, :], ident[:])
+                        nc.tensor.transpose(
+                            bank_words[:, u, b_in_bank * P : (b_in_bank + 1) * P], x_words[:, u, :], ident[:]
+                        )
                 banks.append(bank)
             banks_of_pass[g] = banks
 
         def bank_values(bank):
-            return bank[:].bitcast(BF16).rearrange("p (u n e) -> p n u e", u=PAIR, e=PAIR)
+            return bank[:].bitcast(BF16).rearrange("p (n t) -> p n t", t=PACK)
 
         def scalar_pass(g):
+            if not is_pass(g):
+                return
             planes = work.tile([P, PACK, TOKENS], BF16)
             for half in range(BANKS_PER_PASS):
                 for t in range(PACK):
                     nc.scalar.activation(
                         out=planes[:, t, half * BANK_TOKENS : (half + 1) * BANK_TOKENS],
-                        in_=bank_values(banks_of_pass[g][half])[:, :, t // PAIR, t % PAIR],
+                        in_=bank_values(banks_of_pass[g][half])[:, :, t],
                         func=ACT.Identity,
                         bias=neg_d_last[:, g * PACK + t : g * PACK + t + 1],
                         scale=1.0,
                     )
             planes_of_pass[g] = planes
-            u_raw = u_of_load[g // PASSES_PER_LOAD]
-            u_grouped = work.tile([P, SOURCES, RANK, PACK], BF16, align_bytes=64)
+            u_grouped = ahead.tile([P, SOURCES, RANK, PACK], BF16, align_bytes=64)
             for s in range(SOURCES):
                 nc.scalar.copy(
                     out=u_grouped[:, s].rearrange("p (c i) t -> p c t i", i=4),
-                    in_=u_raw[:, s, g % PASSES_PER_LOAD].rearrange("p (t c i) -> p c t i", t=PACK, i=4),
+                    in_=u_of_pass[g][:, s].rearrange("p (t c i) -> p c t i", t=PACK, i=4),
                 )
             u_grouped_of_pass[g] = u_grouped
 
         def interleave_last(g):
-            diff_last = single.tile([P, TOKENS, PACK], BF16, align_bytes=64)
+            if not is_pass(g):
+                return
+            diff_last = work.tile([P, TOKENS, PACK], BF16, align_bytes=64)
             nc.gpsimd.tensor_scalar(
                 out=diff_last[:],
                 in0=planes_of_pass[g][:].rearrange("p t n -> p n t"),
@@ -128,24 +137,22 @@ def tile_moe_pa_k_kernel(tc, encodings, domain_encs, Us, out):
             diff_last_of_pass[g] = diff_last
 
         def subtract_pass(g):
+            if not is_pass(g):
+                return
             diff = work.tile([P, LAST, TOKENS, PACK], BF16, align_bytes=64)
+            shape = [P, LAST, BANK_TOKENS, PACK]
             for half in range(BANKS_PER_PASS):
-                for s in range(LAST):
-                    d_col = (s * PASSES + g) * PACK
-                    nc.vector.tensor_tensor(
-                        out=diff[:, s, half * BANK_TOKENS : (half + 1) * BANK_TOKENS, :].rearrange(
-                            "p n (u e) -> p n u e", e=PAIR
-                        ),
-                        in0=bank_values(banks_of_pass[g][half]),
-                        in1=d_cols[:, d_col : d_col + PACK]
-                        .rearrange("p (u e) -> p u e", e=PAIR)
-                        .unsqueeze(1)
-                        .to_broadcast([P, BANK_TOKENS, PAIR, PAIR]),
-                        op=ALU.subtract,
-                    )
+                nc.vector.tensor_tensor(
+                    out=diff[:, :, half * BANK_TOKENS : (half + 1) * BANK_TOKENS, :],
+                    in0=bank_values(banks_of_pass[g][half]).unsqueeze(1).to_broadcast(shape),
+                    in1=d_cols[:, 0:LAST, g, :].unsqueeze(2).to_broadcast(shape),
+                    op=ALU.subtract,
+                )
             diff_of_pass[g] = diff
 
         def quantise_pass(g):
+            if not is_pass(g):
+                return
             u_codes = work.tile([P, SOURCES * RANK], U32, align_bytes=64)
             u_scales = work.tile([P, SOURCES * RANK], U8, align_bytes=64)
             nc.vector.quantize_mx(
@@ -165,6 +172,8 @@ def tile_moe_pa_k_kernel(tc, encodings, domain_encs, Us, out):
             codes_of_pass[g] = (u_codes, u_scales, diff_codes, diff_scales)
 
         def multiply_pass(g):
+            if not is_pass(g):
+                return
             u_codes, u_scales, diff_codes, diff_scales = codes_of_pass[g]
             for s in range(SOURCES):
                 nc.tensor.matmul_mx(
@@ -179,8 +188,6 @@ def tile_moe_pa_k_kernel(tc, encodings, domain_encs, Us, out):
 
         d_rows = const.tile([P, K_PASS], BF16)
         nc.sync.dma_start(out=d_rows[:], in_=domain_encs.rearrange("s (g k) -> (s g) k", k=K_PASS))
-        for round_ in range(LOADS_AHEAD):
-            load(round_)
 
         ident = const.tile([P, P], F32)
         make_identity(nc, ident[:])
@@ -196,15 +203,15 @@ def tile_moe_pa_k_kernel(tc, encodings, domain_encs, Us, out):
         d_bank = bank_pool.tile([P, BANK_WORDS], F32, tag="bank")
         for u in range(PAIR):
             nc.tensor.transpose(d_bank[:, u * P : (u + 1) * P], d_words[:, u, :], ident[:])
-        d_cols = const.tile([P, SOURCES * PASSES * PACK], BF16)
+        d_cols = const.tile([P, SOURCES, PASSES, PACK], BF16)
         nc.vector.tensor_copy(
-            out=d_cols[:].bitcast(F32).rearrange("p (r u) -> p r u", u=PAIR),
+            out=d_cols[:].rearrange("p s g t -> p (s g t)").bitcast(F32).rearrange("p (r u) -> p r u", u=PAIR),
             in_=d_bank[:, 0 : PAIR * P].rearrange("p (u r) -> p r u", u=PAIR),
         )
         neg_d_last = const.tile([P, PASSES * PACK], F32)
         nc.vector.tensor_scalar(
             out=neg_d_last[:],
-            in0=d_cols[:, LAST * PASSES * PACK : SOURCES * PASSES * PACK],
+            in0=d_cols[:, LAST].rearrange("p g t -> p (g t)"),
             scalar1=-1.0,
             scalar2=None,
             op0=ALU.mult,
@@ -212,21 +219,14 @@ def tile_moe_pa_k_kernel(tc, encodings, domain_encs, Us, out):
 
         acc = [acc_pool.tile([P, TOKENS], F32, name="acc%d" % s) for s in range(SOURCES)]
 
-        transpose_pass(0)
-        transpose_pass(1)
-        scalar_pass(0)
-        for g in range(PASSES):
-            round_ = g // PASSES_PER_LOAD + LOADS_AHEAD
-            if g % PASSES_PER_LOAD == 0 and round_ < LOADS:
-                load(round_)
-            interleave_last(g)
-            subtract_pass(g)
-            if g + 2 < PASSES:
-                transpose_pass(g + 2)
-            if g + 1 < PASSES:
-                scalar_pass(g + 1)
-            quantise_pass(g)
-            multiply_pass(g)
+        for step in range(PASSES + MULTIPLY_LAG):
+            load(step)
+            interleave_last(step - SUBTRACT_LAG)
+            subtract_pass(step - SUBTRACT_LAG)
+            transpose_pass(step - TRANSPOSE_LAG)
+            scalar_pass(step - SCALAR_LAG)
+            quantise_pass(step - MULTIPLY_LAG)
+            multiply_pass(step - MULTIPLY_LAG)
 
         dist2 = bank_pool.tile([P, BANK_WORDS], F32, tag="bank")
         n_cols = SOURCES * TOKEN_BLOCKS

@@ -28,11 +28,12 @@ BANK_WORDS = 512
 BANK_TOKENS = BANK_WORDS // PAIR
 BANKS_PER_PASS = TOKENS // BANK_TOKENS
 BLOCKS_PER_BANK = BANK_TOKENS // P
+
 TRANSPOSE_LAG = 2
+SUBTRACT_LAG = 3
 SCALAR_LAG = 3
-SUBTRACT_LAG = 4
+INTERLEAVE_LAG = 4
 MULTIPLY_LAG = 5
-ONES_COLS = 2
 
 FLOPS = 2 * SOURCES * TOKENS * HIDDEN * RANK
 
@@ -41,9 +42,7 @@ def tile_moe_pa_k_kernel(tc, encodings, domain_encs, Us, out):
     nc = tc.nc
     with ExitStack() as ctx:
         const = ctx.enter_context(tc.tile_pool(name="const", bufs=1))
-        loads = ctx.enter_context(tc.tile_pool(name="loads", bufs=SCALAR_LAG + 1))
         work = ctx.enter_context(tc.tile_pool(name="work", bufs=2))
-        ahead = ctx.enter_context(tc.tile_pool(name="ahead", bufs=MULTIPLY_LAG - SCALAR_LAG + 1))
         acc_pool = ctx.enter_context(tc.psum_pool(name="acc", bufs=1))
         bank_pool = ctx.enter_context(tc.psum_pool(name="banks", bufs=2 * BANKS_PER_PASS))
         ctx.enter_context(tc.manual_schedule())
@@ -64,45 +63,67 @@ def tile_moe_pa_k_kernel(tc, encodings, domain_encs, Us, out):
             if not is_pass(g):
                 return
             k_lo = g * K_PASS
-            x_sb = loads.tile([P, TOKEN_BLOCKS, K_PASS], BF16)
-            nc.sync.dma_start(
-                out=x_sb[:],
-                in_=encodings[:, k_lo : k_lo + K_PASS].rearrange("(b n) k -> n b k", n=P),
-            )
-            u_raw = loads.tile([P, SOURCES, PACK * RANK], BF16)
+            x_of_pass[g] = []
+            for half in range(BANKS_PER_PASS):
+                x_sb = work.tile([P, BLOCKS_PER_BANK, K_PASS], BF16, bufs=BANKS_PER_PASS * (TRANSPOSE_LAG + 1))
+                nc.sync.dma_start(
+                    out=x_sb[:],
+                    in_=encodings[half * BANK_TOKENS : (half + 1) * BANK_TOKENS, k_lo : k_lo + K_PASS].rearrange(
+                        "(b n) k -> n b k", n=P
+                    ),
+                )
+                x_of_pass[g].append(x_sb)
+            u_raw = work.tile([P, SOURCES, PACK * RANK], BF16, bufs=SCALAR_LAG + 1)
             nc.sync.dma_start(
                 out=u_raw[:],
                 in_=Us[:, k_lo : k_lo + K_PASS, :].rearrange("s (p t) r -> p s (t r)", t=PACK),
             )
-            x_of_pass[g] = x_sb
             u_of_pass[g] = u_raw
 
         def transpose_pass(g):
             if not is_pass(g):
                 return
-            banks = []
+            banks_of_pass[g] = []
             for half in range(BANKS_PER_PASS):
                 bank = bank_pool.tile([P, BANK_WORDS], F32, tag="bank")
                 bank_words = bank[:].rearrange("p (n u) -> p u n", u=PAIR)
-                for b_in_bank in range(BLOCKS_PER_BANK):
-                    x_words = (
-                        x_of_pass[g][:, half * BLOCKS_PER_BANK + b_in_bank, :]
-                        .bitcast(F32)
-                        .rearrange("n (w u) -> n u w", u=PAIR)
-                    )
+                for b in range(BLOCKS_PER_BANK):
+                    x_words = x_of_pass[g][half][:, b, :].bitcast(F32).rearrange("n (w u) -> n u w", u=PAIR)
                     for u in range(PAIR):
-                        nc.tensor.transpose(
-                            bank_words[:, u, b_in_bank * P : (b_in_bank + 1) * P], x_words[:, u, :], ident[:]
-                        )
-                banks.append(bank)
-            banks_of_pass[g] = banks
+                        nc.tensor.transpose(bank_words[:, u, b * P : (b + 1) * P], x_words[:, u, :], ident[:])
+                banks_of_pass[g].append(bank)
 
         def bank_values(bank):
             return bank[:].bitcast(BF16).rearrange("p (n t) -> p n t", t=PACK)
 
+        def subtract_pass(g):
+            if not is_pass(g):
+                return
+            diff = work.tile(
+                [P, LAST, TOKENS, PACK], BF16, align_bytes=64, bufs=MULTIPLY_LAG - SUBTRACT_LAG + 1
+            )
+            shape = [P, LAST, BANK_TOKENS, PACK]
+            for half in range(BANKS_PER_PASS):
+                nc.vector.tensor_tensor(
+                    out=diff[:, :, half * BANK_TOKENS : (half + 1) * BANK_TOKENS, :],
+                    in0=bank_values(banks_of_pass[g][half]).unsqueeze(1).to_broadcast(shape),
+                    in1=d_cols[:, 0:LAST, g, :].unsqueeze(2).to_broadcast(shape),
+                    op=ALU.subtract,
+                )
+            diff_of_pass[g] = diff
+
         def scalar_pass(g):
             if not is_pass(g):
                 return
+            u_grouped = work.tile(
+                [P, SOURCES, RANK, PACK], BF16, align_bytes=64, bufs=MULTIPLY_LAG - SCALAR_LAG + 1
+            )
+            for s in range(SOURCES):
+                nc.scalar.copy(
+                    out=u_grouped[:, s].rearrange("p (c i) t -> p c t i", i=4),
+                    in_=u_of_pass[g][:, s].rearrange("p (t c i) -> p c t i", t=PACK, i=4),
+                )
+            u_grouped_of_pass[g] = u_grouped
             planes = work.tile([P, PACK, TOKENS], BF16)
             for half in range(BANKS_PER_PASS):
                 for t in range(PACK):
@@ -114,18 +135,13 @@ def tile_moe_pa_k_kernel(tc, encodings, domain_encs, Us, out):
                         scale=1.0,
                     )
             planes_of_pass[g] = planes
-            u_grouped = ahead.tile([P, SOURCES, RANK, PACK], BF16, align_bytes=64)
-            for s in range(SOURCES):
-                nc.scalar.copy(
-                    out=u_grouped[:, s].rearrange("p (c i) t -> p c t i", i=4),
-                    in_=u_of_pass[g][:, s].rearrange("p (t c i) -> p c t i", t=PACK, i=4),
-                )
-            u_grouped_of_pass[g] = u_grouped
 
         def interleave_last(g):
             if not is_pass(g):
                 return
-            diff_last = work.tile([P, TOKENS, PACK], BF16, align_bytes=64)
+            diff_last = work.tile(
+                [P, TOKENS, PACK], BF16, align_bytes=64, bufs=MULTIPLY_LAG - INTERLEAVE_LAG + 1
+            )
             nc.gpsimd.tensor_scalar(
                 out=diff_last[:],
                 in0=planes_of_pass[g][:].rearrange("p t n -> p n t"),
@@ -135,20 +151,6 @@ def tile_moe_pa_k_kernel(tc, encodings, domain_encs, Us, out):
                 op1=ALU.add,
             )
             diff_last_of_pass[g] = diff_last
-
-        def subtract_pass(g):
-            if not is_pass(g):
-                return
-            diff = work.tile([P, LAST, TOKENS, PACK], BF16, align_bytes=64)
-            shape = [P, LAST, BANK_TOKENS, PACK]
-            for half in range(BANKS_PER_PASS):
-                nc.vector.tensor_tensor(
-                    out=diff[:, :, half * BANK_TOKENS : (half + 1) * BANK_TOKENS, :],
-                    in0=bank_values(banks_of_pass[g][half]).unsqueeze(1).to_broadcast(shape),
-                    in1=d_cols[:, 0:LAST, g, :].unsqueeze(2).to_broadcast(shape),
-                    op=ALU.subtract,
-                )
-            diff_of_pass[g] = diff
 
         def quantise_pass(g):
             if not is_pass(g):
@@ -191,8 +193,6 @@ def tile_moe_pa_k_kernel(tc, encodings, domain_encs, Us, out):
 
         ident = const.tile([P, P], F32)
         make_identity(nc, ident[:])
-        ones = const.tile([P, ONES_COLS], F32)
-        nc.vector.memset(ones[:], 1.0)
         alphas = const.tile([P, P], F32)
         nc.vector.memset(alphas[:], 0.0)
         warm = const.tile([P, 1], F32)
@@ -221,34 +221,27 @@ def tile_moe_pa_k_kernel(tc, encodings, domain_encs, Us, out):
 
         for step in range(PASSES + MULTIPLY_LAG):
             load(step)
-            interleave_last(step - SUBTRACT_LAG)
-            subtract_pass(step - SUBTRACT_LAG)
+            interleave_last(step - INTERLEAVE_LAG)
             transpose_pass(step - TRANSPOSE_LAG)
+            subtract_pass(step - SUBTRACT_LAG)
             scalar_pass(step - SCALAR_LAG)
             quantise_pass(step - MULTIPLY_LAG)
             multiply_pass(step - MULTIPLY_LAG)
 
-        dist2 = bank_pool.tile([P, BANK_WORDS], F32, tag="bank")
-        n_cols = SOURCES * TOKEN_BLOCKS
+        dist2 = const.tile([P, SOURCES, TOKEN_BLOCKS], F32)
         for s in range(SOURCES):
             squares = const.tile([P, TOKENS], F32, name="squares%d" % s)
             nc.scalar.activation(out=squares[:], in_=acc[s][:], func=ACT.Square)
+            turned = bank_pool.tile([P, BANK_WORDS], F32, tag="bank")
             for b in range(TOKEN_BLOCKS):
-                col = (s * TOKEN_BLOCKS + b) * ONES_COLS
-                nc.tensor.matmul(
-                    out=dist2[:, col : col + ONES_COLS],
-                    lhsT=squares[:, b * P : (b + 1) * P],
-                    rhs=ones[:],
-                    start=True,
-                    stop=True,
-                )
+                nc.tensor.transpose(turned[:, b * P : (b + 1) * P], squares[:, b * P : (b + 1) * P], ident[:])
+            nc.vector.tensor_reduce(
+                out=dist2[:, s, :], in_=turned[:].rearrange("p (b r) -> p b r", r=RANK), axis=AXIS.X, op=ALU.add
+            )
 
         dist = const.tile([P, SOURCES, TOKEN_BLOCKS], F32)
-        nc.scalar.activation(
-            out=dist[:].rearrange("p s b -> p (s b)"),
-            in_=dist2[:, 0 : n_cols * ONES_COLS].rearrange("p (c o) -> p c o", o=ONES_COLS)[:, :, 0],
-            func=ACT.Sqrt,
-        )
+        nc.scalar.activation(out=dist[:], in_=dist2[:], func=ACT.Sqrt)
+        nc.scalar.activation(out=warm[:], in_=warm[:], func=ACT.Exp)
         nearest = const.tile([P, TOKEN_BLOCKS], F32)
         nc.vector.tensor_reduce(out=nearest[:], in_=dist[:].rearrange("p s b -> p b s"), axis=AXIS.X, op=ALU.min)
         excess = const.tile([P, SOURCES, TOKEN_BLOCKS], F32)
@@ -264,8 +257,9 @@ def tile_moe_pa_k_kernel(tc, encodings, domain_encs, Us, out):
         nc.vector.tensor_reduce(out=total[:], in_=weights[:].rearrange("p s b -> p b s"), axis=AXIS.X, op=ALU.add)
         inv_total = const.tile([P, TOKEN_BLOCKS], F32)
         nc.vector.reciprocal(out=inv_total[:], in_=total[:])
+        n_rows = SOURCES * TOKEN_BLOCKS
         nc.vector.tensor_tensor(
-            out=alphas[:, 0:n_cols].rearrange("p (s b) -> p s b", s=SOURCES),
+            out=alphas[:, 0:n_rows].rearrange("p (s b) -> p s b", s=SOURCES),
             in0=weights[:],
             in1=inv_total[:].unsqueeze(1).to_broadcast([P, SOURCES, TOKEN_BLOCKS]),
             op=ALU.mult,
@@ -274,4 +268,4 @@ def tile_moe_pa_k_kernel(tc, encodings, domain_encs, Us, out):
         nc.tensor.transpose(alphas_bank[:, 0:P], alphas[:], ident[:])
         alphas_rows = const.tile([P, P], F32)
         nc.vector.tensor_copy(out=alphas_rows[:], in_=alphas_bank[:, 0:P])
-        nc.sync.dma_start(out=out.rearrange("s (b n) -> (s b) n", n=P), in_=alphas_rows[0:n_cols, :])
+        nc.sync.dma_start(out=out.rearrange("s (b n) -> (s b) n", n=P), in_=alphas_rows[0:n_rows, :])

@@ -34,6 +34,10 @@ SUBTRACT_LAG = 3
 SCALAR_LAG = 3
 INTERLEAVE_LAG = 4
 MULTIPLY_LAG = 5
+MATMUL_LAG = 3
+
+MM_TOKENS = 68
+MM_ROWS = P - LAST
 
 FLOPS = 2 * SOURCES * TOKENS * HIDDEN * RANK
 
@@ -44,7 +48,8 @@ def tile_moe_pa_k_kernel(tc, encodings, domain_encs, Us, out):
         const = ctx.enter_context(tc.tile_pool(name="const", bufs=1))
         work = ctx.enter_context(tc.tile_pool(name="work", bufs=2))
         acc_pool = ctx.enter_context(tc.psum_pool(name="acc", bufs=1))
-        bank_pool = ctx.enter_context(tc.psum_pool(name="banks", bufs=2 * BANKS_PER_PASS))
+        bank_pool = ctx.enter_context(tc.psum_pool(name="banks", bufs=3))
+        mm_pool = ctx.enter_context(tc.psum_pool(name="mm", bufs=1))
         ctx.enter_context(tc.manual_schedule())
 
         x_of_pass = {}
@@ -55,6 +60,8 @@ def tile_moe_pa_k_kernel(tc, encodings, domain_encs, Us, out):
         diff_of_pass = {}
         diff_last_of_pass = {}
         codes_of_pass = {}
+        rows_of_pass = {}
+        mm_bank_of_pass = {}
 
         def is_pass(g):
             return 0 <= g < PASSES
@@ -79,19 +86,42 @@ def tile_moe_pa_k_kernel(tc, encodings, domain_encs, Us, out):
                 in_=Us[:, k_lo : k_lo + K_PASS, :].rearrange("s (p t) r -> p s (t r)", t=PACK),
             )
             u_of_pass[g] = u_raw
+            load_rows(g)
 
-        def transpose_pass(g):
+        def load_rows(g):
+            k_lo = g * K_PASS
+            k_hi = k_lo + K_PASS
+            rows = work.tile([P, K_PASS], BF16, bufs=MATMUL_LAG + 1)
+            nc.sync.dma_start(out=rows[0:MM_ROWS, :], in_=encodings[0:MM_ROWS, k_lo:k_hi])
+            nc.sync.dma_start(out=rows[MM_ROWS:P, :], in_=domain_encs[0:LAST, k_lo:k_hi])
+            rows_of_pass[g] = rows
+
+        def matmul_pass(g):
             if not is_pass(g):
                 return
-            banks_of_pass[g] = []
-            for half in range(BANKS_PER_PASS):
-                bank = bank_pool.tile([P, BANK_WORDS], F32, tag="bank")
-                bank_words = bank[:].rearrange("p (n u) -> p u n", u=PAIR)
-                for b in range(BLOCKS_PER_BANK):
-                    x_words = x_of_pass[g][half][:, b, :].bitcast(F32).rearrange("n (w u) -> n u w", u=PAIR)
-                    for u in range(PAIR):
-                        nc.tensor.transpose(bank_words[:, u, b * P : (b + 1) * P], x_words[:, u, :], ident[:])
-                banks_of_pass[g].append(bank)
+            mm_bank = mm_pool.tile([P, 2 * BANK_WORDS], BF16)
+            values = mm_bank[:, 0 : PACK * LAST * MM_TOKENS].rearrange("p (t c) -> p t c", t=PACK)
+            rows = rows_of_pass[g][:].rearrange("n (m t) -> n t m", t=PACK)
+            for t in range(PACK):
+                nc.tensor.matmul(
+                    values[:, t, :],
+                    lhsT=rows[:, t, :],
+                    rhs=pick[:].rearrange("p s n -> p (s n)"),
+                    start=True,
+                    stop=True,
+                )
+            mm_bank_of_pass[g] = mm_bank
+
+        def transpose_half(g, half):
+            if not is_pass(g):
+                return
+            bank = bank_pool.tile([P, BANK_WORDS], F32, tag="bank")
+            bank_words = bank[:].rearrange("p (n u) -> p u n", u=PAIR)
+            for b in range(BLOCKS_PER_BANK):
+                x_words = x_of_pass[g][half][:, b, :].bitcast(F32).rearrange("n (w u) -> n u w", u=PAIR)
+                for u in range(PAIR):
+                    nc.tensor.transpose(bank_words[:, u, b * P : (b + 1) * P], x_words[:, u, :], ident[:])
+            banks_of_pass.setdefault(g, []).append(bank)
 
         def bank_values(bank):
             return bank[:].bitcast(BF16).rearrange("p (n t) -> p n t", t=PACK)
@@ -102,11 +132,12 @@ def tile_moe_pa_k_kernel(tc, encodings, domain_encs, Us, out):
             diff = work.tile(
                 [P, LAST, TOKENS, PACK], BF16, align_bytes=64, bufs=MULTIPLY_LAG - SUBTRACT_LAG + 1
             )
-            shape = [P, LAST, BANK_TOKENS, PACK]
             for half in range(BANKS_PER_PASS):
+                skip = MM_TOKENS if half == 0 else 0
+                shape = [P, LAST, BANK_TOKENS - skip, PACK]
                 nc.vector.tensor_tensor(
-                    out=diff[:, :, half * BANK_TOKENS : (half + 1) * BANK_TOKENS, :],
-                    in0=bank_values(banks_of_pass[g][half]).unsqueeze(1).to_broadcast(shape),
+                    out=diff[:, :, half * BANK_TOKENS + skip : (half + 1) * BANK_TOKENS, :],
+                    in0=bank_values(banks_of_pass[g][half])[:, skip:, :].unsqueeze(1).to_broadcast(shape),
                     in1=d_cols[:, 0:LAST, g, :].unsqueeze(2).to_broadcast(shape),
                     op=ALU.subtract,
                 )
@@ -124,6 +155,10 @@ def tile_moe_pa_k_kernel(tc, encodings, domain_encs, Us, out):
                     in_=u_of_pass[g][:, s].rearrange("p (t c i) -> p c t i", t=PACK, i=4),
                 )
             u_grouped_of_pass[g] = u_grouped
+            nc.scalar.copy(
+                out=diff_of_pass[g][:, :, 0:MM_TOKENS, :],
+                in_=mm_bank_of_pass[g][:, 0 : PACK * LAST * MM_TOKENS].rearrange("p (t s n) -> p s n t", s=LAST, t=PACK),
+            )
             planes = work.tile([P, PACK, TOKENS], BF16)
             for half in range(BANKS_PER_PASS):
                 for t in range(PACK):
@@ -199,6 +234,14 @@ def tile_moe_pa_k_kernel(tc, encodings, domain_encs, Us, out):
         nc.vector.memset(warm[:], 1.0)
         nc.scalar.activation(out=warm[:], in_=warm[:], func=ACT.Sqrt)
 
+        pick = const.tile([P, LAST, MM_TOKENS], BF16)
+        nc.vector.tensor_tensor(
+            out=pick[:],
+            in0=ident[:, 0:MM_TOKENS].unsqueeze(1).to_broadcast([P, LAST, MM_TOKENS]),
+            in1=ident[:, MM_ROWS:P].unsqueeze(2).to_broadcast([P, LAST, MM_TOKENS]),
+            op=ALU.subtract,
+        )
+
         d_words = d_rows[:].bitcast(F32).rearrange("r (w u) -> r u w", u=PAIR)
         d_bank = bank_pool.tile([P, BANK_WORDS], F32, tag="bank")
         for u in range(PAIR):
@@ -222,9 +265,11 @@ def tile_moe_pa_k_kernel(tc, encodings, domain_encs, Us, out):
         for step in range(PASSES + MULTIPLY_LAG):
             load(step)
             interleave_last(step - INTERLEAVE_LAG)
-            transpose_pass(step - TRANSPOSE_LAG)
+            transpose_half(step - TRANSPOSE_LAG, 0)
+            matmul_pass(step - MATMUL_LAG)
             subtract_pass(step - SUBTRACT_LAG)
             scalar_pass(step - SCALAR_LAG)
+            transpose_half(step - TRANSPOSE_LAG, 1)
             quantise_pass(step - MULTIPLY_LAG)
             multiply_pass(step - MULTIPLY_LAG)
 

@@ -32,12 +32,14 @@ BLOCKS_PER_BANK = BANK_TOKENS // P
 TRANSPOSE_LAG = 2
 SUBTRACT_LAG = 3
 SCALAR_LAG = 3
-INTERLEAVE_LAG = 4
-MULTIPLY_LAG = 5
+INTERLEAVE_LAG = 5
+MULTIPLY_LAG = 6
 MATMUL_LAG = 3
 
-MM_TOKENS = 68
-MM_ROWS = P - LAST
+MM_TOKENS = 60
+MM_TOKENS_LAST = 24
+MM_COLS = LAST * MM_TOKENS + MM_TOKENS_LAST
+MM_ROWS = P - SOURCES
 
 FLOPS = 2 * SOURCES * TOKENS * HIDDEN * RANK
 
@@ -93,20 +95,20 @@ def tile_moe_pa_k_kernel(tc, encodings, domain_encs, Us, out):
             k_hi = k_lo + K_PASS
             rows = work.tile([P, K_PASS], BF16, bufs=MATMUL_LAG + 1)
             nc.sync.dma_start(out=rows[0:MM_ROWS, :], in_=encodings[0:MM_ROWS, k_lo:k_hi])
-            nc.sync.dma_start(out=rows[MM_ROWS:P, :], in_=domain_encs[0:LAST, k_lo:k_hi])
+            nc.sync.dma_start(out=rows[MM_ROWS:P, :], in_=domain_encs[:, k_lo:k_hi])
             rows_of_pass[g] = rows
 
         def matmul_pass(g):
             if not is_pass(g):
                 return
             mm_bank = mm_pool.tile([P, 2 * BANK_WORDS], BF16)
-            values = mm_bank[:, 0 : PACK * LAST * MM_TOKENS].rearrange("p (t c) -> p t c", t=PACK)
+            values = mm_bank[:, 0 : PACK * MM_COLS].rearrange("p (t c) -> p t c", t=PACK)
             rows = rows_of_pass[g][:].rearrange("n (m t) -> n t m", t=PACK)
             for t in range(PACK):
                 nc.tensor.matmul(
                     values[:, t, :],
                     lhsT=rows[:, t, :],
-                    rhs=pick[:].rearrange("p s n -> p (s n)"),
+                    rhs=pick[:],
                     start=True,
                     stop=True,
                 )
@@ -155,16 +157,19 @@ def tile_moe_pa_k_kernel(tc, encodings, domain_encs, Us, out):
                     in_=u_of_pass[g][:, s].rearrange("p (t c i) -> p c t i", t=PACK, i=4),
                 )
             u_grouped_of_pass[g] = u_grouped
+            mm_values = mm_bank_of_pass[g][:, 0 : PACK * MM_COLS].rearrange("p (t c) -> p t c", t=PACK)
             nc.scalar.copy(
                 out=diff_of_pass[g][:, :, 0:MM_TOKENS, :],
-                in_=mm_bank_of_pass[g][:, 0 : PACK * LAST * MM_TOKENS].rearrange("p (t s n) -> p s n t", s=LAST, t=PACK),
+                in_=mm_values[:, :, 0 : LAST * MM_TOKENS].rearrange("p t (s n) -> p s n t", s=LAST),
             )
-            planes = work.tile([P, PACK, TOKENS], BF16)
+            planes = work.tile([P, PACK, TOKENS], BF16, bufs=INTERLEAVE_LAG - SCALAR_LAG + 1)
+            nc.scalar.copy(out=planes[:, :, 0:MM_TOKENS_LAST], in_=mm_values[:, :, LAST * MM_TOKENS : MM_COLS])
             for half in range(BANKS_PER_PASS):
+                skip = MM_TOKENS_LAST if half == 0 else 0
                 for t in range(PACK):
                     nc.scalar.activation(
-                        out=planes[:, t, half * BANK_TOKENS : (half + 1) * BANK_TOKENS],
-                        in_=bank_values(banks_of_pass[g][half])[:, :, t],
+                        out=planes[:, t, half * BANK_TOKENS + skip : (half + 1) * BANK_TOKENS],
+                        in_=bank_values(banks_of_pass[g][half])[:, skip:, t],
                         func=ACT.Identity,
                         bias=neg_d_last[:, g * PACK + t : g * PACK + t + 1],
                         scale=1.0,
@@ -199,12 +204,15 @@ def tile_moe_pa_k_kernel(tc, encodings, domain_encs, Us, out):
             )
             diff_codes = work.tile([P, SOURCES, TOKENS], U32, align_bytes=64)
             diff_scales = work.tile([P, SOURCES, TOKENS], U8, align_bytes=64)
-            for s in range(SOURCES):
-                values = diff_of_pass[g][:, s] if s < LAST else diff_last_of_pass[g][:]
+            for values, lo, hi in (
+                (diff_of_pass[g][:, 0:2].rearrange("p s n t -> p (s n t)"), 0, 2),
+                (diff_last_of_pass[g][:].rearrange("p n t -> p (n t)"), LAST, SOURCES),
+                (diff_of_pass[g][:, 2].rearrange("p n t -> p (n t)"), 2, LAST),
+            ):
                 nc.vector.quantize_mx(
-                    out=diff_codes[:, s, :].bitcast(FP8X4),
-                    scales=diff_scales[:, s, :],
-                    in_=values.rearrange("p n t -> p (n t)"),
+                    out=diff_codes[:, lo:hi, :].rearrange("p s n -> p (s n)").bitcast(FP8X4),
+                    scales=diff_scales[:, lo:hi, :].rearrange("p s n -> p (s n)"),
+                    in_=values,
                 )
             codes_of_pass[g] = (u_codes, u_scales, diff_codes, diff_scales)
 
@@ -234,11 +242,17 @@ def tile_moe_pa_k_kernel(tc, encodings, domain_encs, Us, out):
         nc.vector.memset(warm[:], 1.0)
         nc.scalar.activation(out=warm[:], in_=warm[:], func=ACT.Sqrt)
 
-        pick = const.tile([P, LAST, MM_TOKENS], BF16)
+        pick = const.tile([P, MM_COLS], BF16)
         nc.vector.tensor_tensor(
-            out=pick[:],
+            out=pick[:, 0 : LAST * MM_TOKENS].rearrange("p (s n) -> p s n", s=LAST),
             in0=ident[:, 0:MM_TOKENS].unsqueeze(1).to_broadcast([P, LAST, MM_TOKENS]),
-            in1=ident[:, MM_ROWS:P].unsqueeze(2).to_broadcast([P, LAST, MM_TOKENS]),
+            in1=ident[:, MM_ROWS : MM_ROWS + LAST].unsqueeze(2).to_broadcast([P, LAST, MM_TOKENS]),
+            op=ALU.subtract,
+        )
+        nc.vector.tensor_tensor(
+            out=pick[:, LAST * MM_TOKENS : MM_COLS],
+            in0=ident[:, 0:MM_TOKENS_LAST],
+            in1=ident[:, MM_ROWS + LAST : P].to_broadcast([P, MM_TOKENS_LAST]),
             op=ALU.subtract,
         )
 

@@ -32,14 +32,15 @@ BLOCKS_PER_BANK = BANK_TOKENS // P
 TRANSPOSE_LAG = 2
 SUBTRACT_LAG = 3
 SCALAR_LAG = 3
-INTERLEAVE_LAG = 5
-MULTIPLY_LAG = 6
+INTERLEAVE_LAG = 4
+MULTIPLY_LAG = 5
 MATMUL_LAG = 3
 
 MM_TOKENS = 60
 MM_TOKENS_LAST = 24
 MM_COLS = LAST * MM_TOKENS + MM_TOKENS_LAST
-MM_ROWS = P - SOURCES
+MM_ROWS = 64
+MM_TILES = MATMUL_LAG + 1
 
 FLOPS = 2 * SOURCES * TOKENS * HIDDEN * RANK
 
@@ -62,7 +63,6 @@ def tile_moe_pa_k_kernel(tc, encodings, domain_encs, Us, out):
         diff_of_pass = {}
         diff_last_of_pass = {}
         codes_of_pass = {}
-        rows_of_pass = {}
         mm_bank_of_pass = {}
 
         def is_pass(g):
@@ -93,17 +93,16 @@ def tile_moe_pa_k_kernel(tc, encodings, domain_encs, Us, out):
         def load_rows(g):
             k_lo = g * K_PASS
             k_hi = k_lo + K_PASS
-            rows = work.tile([P, K_PASS], BF16, bufs=MATMUL_LAG + 1)
+            rows = mm_rows[g % MM_TILES]
             nc.sync.dma_start(out=rows[0:MM_ROWS, :], in_=encodings[0:MM_ROWS, k_lo:k_hi])
-            nc.sync.dma_start(out=rows[MM_ROWS:P, :], in_=domain_encs[:, k_lo:k_hi])
-            rows_of_pass[g] = rows
+            nc.sync.dma_start(out=rows[MM_ROWS : MM_ROWS + SOURCES, :], in_=domain_encs[:, k_lo:k_hi])
 
         def matmul_pass(g):
             if not is_pass(g):
                 return
             mm_bank = mm_pool.tile([P, 2 * BANK_WORDS], BF16)
             values = mm_bank[:, 0 : PACK * MM_COLS].rearrange("p (t c) -> p t c", t=PACK)
-            rows = rows_of_pass[g][:].rearrange("n (m t) -> n t m", t=PACK)
+            rows = mm_rows[g % MM_TILES][:].rearrange("n (m t) -> n t m", t=PACK)
             for t in range(PACK):
                 nc.tensor.matmul(
                     values[:, t, :],
@@ -145,25 +144,10 @@ def tile_moe_pa_k_kernel(tc, encodings, domain_encs, Us, out):
                 )
             diff_of_pass[g] = diff
 
-        def scalar_pass(g):
+        def planes_pass(g):
             if not is_pass(g):
                 return
-            u_grouped = work.tile(
-                [P, SOURCES, RANK, PACK], BF16, align_bytes=64, bufs=MULTIPLY_LAG - SCALAR_LAG + 1
-            )
-            for s in range(SOURCES):
-                nc.scalar.copy(
-                    out=u_grouped[:, s].rearrange("p (c i) t -> p c t i", i=4),
-                    in_=u_of_pass[g][:, s].rearrange("p (t c i) -> p c t i", t=PACK, i=4),
-                )
-            u_grouped_of_pass[g] = u_grouped
-            mm_values = mm_bank_of_pass[g][:, 0 : PACK * MM_COLS].rearrange("p (t c) -> p t c", t=PACK)
-            nc.scalar.copy(
-                out=diff_of_pass[g][:, :, 0:MM_TOKENS, :],
-                in_=mm_values[:, :, 0 : LAST * MM_TOKENS].rearrange("p t (s n) -> p s n t", s=LAST),
-            )
             planes = work.tile([P, PACK, TOKENS], BF16, bufs=INTERLEAVE_LAG - SCALAR_LAG + 1)
-            nc.scalar.copy(out=planes[:, :, 0:MM_TOKENS_LAST], in_=mm_values[:, :, LAST * MM_TOKENS : MM_COLS])
             for half in range(BANKS_PER_PASS):
                 skip = MM_TOKENS_LAST if half == 0 else 0
                 for t in range(PACK):
@@ -175,6 +159,27 @@ def tile_moe_pa_k_kernel(tc, encodings, domain_encs, Us, out):
                         scale=1.0,
                     )
             planes_of_pass[g] = planes
+
+        def scalar_pass(g):
+            if not is_pass(g):
+                return
+            mm_values = mm_bank_of_pass[g][:, 0 : PACK * MM_COLS].rearrange("p (t c) -> p t c", t=PACK)
+            nc.scalar.copy(
+                out=planes_of_pass[g][:, :, 0:MM_TOKENS_LAST], in_=mm_values[:, :, LAST * MM_TOKENS : MM_COLS]
+            )
+            nc.scalar.copy(
+                out=diff_of_pass[g][:, :, 0:MM_TOKENS, :],
+                in_=mm_values[:, :, 0 : LAST * MM_TOKENS].rearrange("p t (s n) -> p s n t", s=LAST),
+            )
+            u_grouped = work.tile(
+                [P, SOURCES, RANK, PACK], BF16, align_bytes=64, bufs=MULTIPLY_LAG - SCALAR_LAG + 1
+            )
+            for s in range(SOURCES):
+                nc.scalar.copy(
+                    out=u_grouped[:, s].rearrange("p (c i) t -> p c t i", i=4),
+                    in_=u_of_pass[g][:, s].rearrange("p (t c i) -> p c t i", t=PACK, i=4),
+                )
+            u_grouped_of_pass[g] = u_grouped
 
         def interleave_last(g):
             if not is_pass(g):
@@ -234,6 +239,10 @@ def tile_moe_pa_k_kernel(tc, encodings, domain_encs, Us, out):
         d_rows = const.tile([P, K_PASS], BF16)
         nc.sync.dma_start(out=d_rows[:], in_=domain_encs.rearrange("s (g k) -> (s g) k", k=K_PASS))
 
+        mm_rows = [const.tile([P, K_PASS], BF16, name="mm_rows%d" % i) for i in range(MM_TILES)]
+        for rows in mm_rows:
+            nc.vector.memset(rows[MM_ROWS:P, :], 0.0)
+
         ident = const.tile([P, P], F32)
         make_identity(nc, ident[:])
         alphas = const.tile([P, P], F32)
@@ -252,7 +261,7 @@ def tile_moe_pa_k_kernel(tc, encodings, domain_encs, Us, out):
         nc.vector.tensor_tensor(
             out=pick[:, LAST * MM_TOKENS : MM_COLS],
             in0=ident[:, 0:MM_TOKENS_LAST],
-            in1=ident[:, MM_ROWS + LAST : P].to_broadcast([P, MM_TOKENS_LAST]),
+            in1=ident[:, MM_ROWS + LAST : MM_ROWS + SOURCES].to_broadcast([P, MM_TOKENS_LAST]),
             op=ALU.subtract,
         )
 
@@ -282,8 +291,9 @@ def tile_moe_pa_k_kernel(tc, encodings, domain_encs, Us, out):
             transpose_half(step - TRANSPOSE_LAG, 0)
             matmul_pass(step - MATMUL_LAG)
             subtract_pass(step - SUBTRACT_LAG)
-            scalar_pass(step - SCALAR_LAG)
+            planes_pass(step - SCALAR_LAG)
             transpose_half(step - TRANSPOSE_LAG, 1)
+            scalar_pass(step - SCALAR_LAG)
             quantise_pass(step - MULTIPLY_LAG)
             multiply_pass(step - MULTIPLY_LAG)
 

@@ -33,13 +33,13 @@ TRANSPOSE_LAG = 2
 SUBTRACT_LAG = 3
 SCALAR_LAG = 3
 INTERLEAVE_LAG = 4
-MULTIPLY_LAG = 5
+MULTIPLY_LAG = 4
 MATMUL_LAG = 3
 
-MM_TOKENS = 60
-MM_TOKENS_LAST = 24
+MM_TOKENS = 40
+MM_TOKENS_LAST = 84
 MM_COLS = LAST * MM_TOKENS + MM_TOKENS_LAST
-MM_ROWS = 64
+MM_ROWS = 96
 MM_TILES = MATMUL_LAG + 1
 
 FLOPS = 2 * SOURCES * TOKENS * HIDDEN * RANK
@@ -94,7 +94,8 @@ def tile_moe_pa_k_kernel(tc, encodings, domain_encs, Us, out):
             k_lo = g * K_PASS
             k_hi = k_lo + K_PASS
             rows = mm_rows[g % MM_TILES]
-            nc.sync.dma_start(out=rows[0:MM_ROWS, :], in_=encodings[0:MM_ROWS, k_lo:k_hi])
+            for lo, hi in ((0, 64), (64, MM_ROWS)):
+                nc.sync.dma_start(out=rows[lo:hi, :], in_=encodings[lo:hi, k_lo:k_hi])
             nc.sync.dma_start(out=rows[MM_ROWS : MM_ROWS + SOURCES, :], in_=domain_encs[:, k_lo:k_hi])
 
         def matmul_pass(g):
@@ -185,7 +186,7 @@ def tile_moe_pa_k_kernel(tc, encodings, domain_encs, Us, out):
             if not is_pass(g):
                 return
             diff_last = work.tile(
-                [P, TOKENS, PACK], BF16, align_bytes=64, bufs=MULTIPLY_LAG - INTERLEAVE_LAG + 1
+                [P, TOKENS, PACK], BF16, align_bytes=64, bufs=1
             )
             nc.gpsimd.tensor_scalar(
                 out=diff_last[:],
@@ -225,7 +226,7 @@ def tile_moe_pa_k_kernel(tc, encodings, domain_encs, Us, out):
             if not is_pass(g):
                 return
             u_codes, u_scales, diff_codes, diff_scales = codes_of_pass[g]
-            for s in range(SOURCES):
+            for s in (0, 1, 3, 2):
                 nc.tensor.matmul_mx(
                     out=acc[s][:],
                     lhsT=u_codes[:, s * RANK : (s + 1) * RANK].bitcast(FP8X4),

@@ -161,17 +161,9 @@ def tile_moe_pa_k_kernel(tc, encodings, domain_encs, Us, out):
                     )
             planes_of_pass[g] = planes
 
-        def scalar_pass(g):
+        def regroup_pass(g):
             if not is_pass(g):
                 return
-            mm_values = mm_bank_of_pass[g][:, 0 : PACK * MM_COLS].rearrange("p (t c) -> p t c", t=PACK)
-            nc.scalar.copy(
-                out=planes_of_pass[g][:, :, 0:MM_TOKENS_LAST], in_=mm_values[:, :, LAST * MM_TOKENS : MM_COLS]
-            )
-            nc.scalar.copy(
-                out=diff_of_pass[g][:, :, 0:MM_TOKENS, :],
-                in_=mm_values[:, :, 0 : LAST * MM_TOKENS].rearrange("p t (s n) -> p s n t", s=LAST),
-            )
             u_grouped = work.tile(
                 [P, SOURCES, RANK, PACK], BF16, align_bytes=64, bufs=MULTIPLY_LAG - SCALAR_LAG + 1
             )
@@ -182,6 +174,19 @@ def tile_moe_pa_k_kernel(tc, encodings, domain_encs, Us, out):
                 )
             u_grouped_of_pass[g] = u_grouped
 
+        def copy_share(g):
+            if not is_pass(g):
+                return
+            mm_values = mm_bank_of_pass[g][:, 0 : PACK * MM_COLS].rearrange("p (t c) -> p t c", t=PACK)
+            nc.scalar.copy(
+                out=diff_of_pass[g][:, :, 0:MM_TOKENS, :],
+                in_=mm_values[:, :, 0 : LAST * MM_TOKENS].rearrange("p t (s n) -> p s n t", s=LAST),
+            )
+            nc.scalar.copy(
+                out=diff_last_of_pass[g][:, 0:MM_TOKENS_LAST, :],
+                in_=mm_values[:, :, LAST * MM_TOKENS : MM_COLS].rearrange("p t n -> p n t"),
+            )
+
         def interleave_last(g):
             if not is_pass(g):
                 return
@@ -189,8 +194,8 @@ def tile_moe_pa_k_kernel(tc, encodings, domain_encs, Us, out):
                 [P, TOKENS, PACK], BF16, align_bytes=64, bufs=1
             )
             nc.gpsimd.tensor_scalar(
-                out=diff_last[:],
-                in0=planes_of_pass[g][:].rearrange("p t n -> p n t"),
+                out=diff_last[:, MM_TOKENS_LAST:, :],
+                in0=planes_of_pass[g][:, :, MM_TOKENS_LAST:].rearrange("p t n -> p n t"),
                 scalar1=1.0,
                 scalar2=0.0,
                 op0=ALU.mult,
@@ -289,12 +294,13 @@ def tile_moe_pa_k_kernel(tc, encodings, domain_encs, Us, out):
         for step in range(PASSES + MULTIPLY_LAG):
             load(step)
             interleave_last(step - INTERLEAVE_LAG)
+            copy_share(step - INTERLEAVE_LAG)
             transpose_half(step - TRANSPOSE_LAG, 0)
             matmul_pass(step - MATMUL_LAG)
             subtract_pass(step - SUBTRACT_LAG)
             planes_pass(step - SCALAR_LAG)
             transpose_half(step - TRANSPOSE_LAG, 1)
-            scalar_pass(step - SCALAR_LAG)
+            regroup_pass(step - SCALAR_LAG)
             quantise_pass(step - MULTIPLY_LAG)
             multiply_pass(step - MULTIPLY_LAG)
 

@@ -15,6 +15,8 @@ AXIS = mybir.AxisListType
 P = 128
 PACK = 4
 K_PASS = P * PACK
+SOURCE_ORDER = (2, 3, 0, 1)
+US_SLOT = 3
 PAIR = 2
 
 TOKENS = 512
@@ -30,16 +32,17 @@ BANKS_PER_PASS = TOKENS // BANK_TOKENS
 BLOCKS_PER_BANK = BANK_TOKENS // P
 
 TRANSPOSE_LAG = 2
+REGROUP_LAG = 2
+MATMUL_LAG = 3
 SUBTRACT_LAG = 3
-SCALAR_LAG = 3
+PLANES_LAG = 3
 INTERLEAVE_LAG = 4
 MULTIPLY_LAG = 4
-MATMUL_LAG = 3
 
-MM_TOKENS = 40
-MM_TOKENS_LAST = 84
+MM_TOKENS = 46
+MM_TOKENS_LAST = 64
 MM_COLS = LAST * MM_TOKENS + MM_TOKENS_LAST
-MM_ROWS = 96
+MM_ROWS = 64
 MM_TILES = MATMUL_LAG + 1
 
 FLOPS = 2 * SOURCES * TOKENS * HIDDEN * RANK
@@ -59,8 +62,7 @@ def tile_moe_pa_k_kernel(tc, encodings, domain_encs, Us, out):
         u_of_pass = {}
         banks_of_pass = {}
         planes_of_pass = {}
-        u_grouped_of_pass = {}
-        diff_of_pass = {}
+        mixed_of_pass = {}
         diff_last_of_pass = {}
         codes_of_pass = {}
         mm_bank_of_pass = {}
@@ -82,7 +84,7 @@ def tile_moe_pa_k_kernel(tc, encodings, domain_encs, Us, out):
                     ),
                 )
                 x_of_pass[g].append(x_sb)
-            u_raw = work.tile([P, SOURCES, PACK * RANK], BF16, bufs=SCALAR_LAG + 1)
+            u_raw = work.tile([P, SOURCES, PACK * RANK], BF16, bufs=REGROUP_LAG + 2)
             nc.sync.dma_start(
                 out=u_raw[:],
                 in_=Us[:, k_lo : k_lo + K_PASS, :].rearrange("s (p t) r -> p s (t r)", t=PACK),
@@ -94,8 +96,7 @@ def tile_moe_pa_k_kernel(tc, encodings, domain_encs, Us, out):
             k_lo = g * K_PASS
             k_hi = k_lo + K_PASS
             rows = mm_rows[g % MM_TILES]
-            for lo, hi in ((0, 64), (64, MM_ROWS)):
-                nc.sync.dma_start(out=rows[lo:hi, :], in_=encodings[lo:hi, k_lo:k_hi])
+            nc.sync.dma_start(out=rows[0:MM_ROWS, :], in_=encodings[0:MM_ROWS, k_lo:k_hi])
             nc.sync.dma_start(out=rows[MM_ROWS : MM_ROWS + SOURCES, :], in_=domain_encs[:, k_lo:k_hi])
 
         def matmul_pass(g):
@@ -131,24 +132,21 @@ def tile_moe_pa_k_kernel(tc, encodings, domain_encs, Us, out):
         def subtract_pass(g):
             if not is_pass(g):
                 return
-            diff = work.tile(
-                [P, LAST, TOKENS, PACK], BF16, align_bytes=64, bufs=MULTIPLY_LAG - SUBTRACT_LAG + 1
-            )
+            diff = mixed_of_pass[g]
             for half in range(BANKS_PER_PASS):
                 skip = MM_TOKENS if half == 0 else 0
                 shape = [P, LAST, BANK_TOKENS - skip, PACK]
                 nc.vector.tensor_tensor(
-                    out=diff[:, :, half * BANK_TOKENS + skip : (half + 1) * BANK_TOKENS, :],
+                    out=diff[:, 0:LAST, half * BANK_TOKENS + skip : (half + 1) * BANK_TOKENS, :],
                     in0=bank_values(banks_of_pass[g][half])[:, skip:, :].unsqueeze(1).to_broadcast(shape),
                     in1=d_cols[:, 0:LAST, g, :].unsqueeze(2).to_broadcast(shape),
                     op=ALU.subtract,
                 )
-            diff_of_pass[g] = diff
 
         def planes_pass(g):
             if not is_pass(g):
                 return
-            planes = work.tile([P, PACK, TOKENS], BF16, bufs=INTERLEAVE_LAG - SCALAR_LAG + 1)
+            planes = work.tile([P, PACK, TOKENS], BF16, bufs=INTERLEAVE_LAG - PLANES_LAG + 1)
             for half in range(BANKS_PER_PASS):
                 skip = MM_TOKENS_LAST if half == 0 else 0
                 for t in range(PACK):
@@ -164,22 +162,23 @@ def tile_moe_pa_k_kernel(tc, encodings, domain_encs, Us, out):
         def regroup_pass(g):
             if not is_pass(g):
                 return
-            u_grouped = work.tile(
-                [P, SOURCES, RANK, PACK], BF16, align_bytes=64, bufs=MULTIPLY_LAG - SCALAR_LAG + 1
+            mixed = work.tile(
+                [P, SOURCES, TOKENS, PACK], BF16, align_bytes=64, bufs=MULTIPLY_LAG - REGROUP_LAG + 1
             )
+            u_grouped = mixed[:, US_SLOT].rearrange("p (s r) t -> p s r t", s=SOURCES)
             for s in range(SOURCES):
                 nc.scalar.copy(
                     out=u_grouped[:, s].rearrange("p (c i) t -> p c t i", i=4),
                     in_=u_of_pass[g][:, s].rearrange("p (t c i) -> p c t i", t=PACK, i=4),
                 )
-            u_grouped_of_pass[g] = u_grouped
+            mixed_of_pass[g] = mixed
 
         def copy_share(g):
             if not is_pass(g):
                 return
             mm_values = mm_bank_of_pass[g][:, 0 : PACK * MM_COLS].rearrange("p (t c) -> p t c", t=PACK)
             nc.scalar.copy(
-                out=diff_of_pass[g][:, :, 0:MM_TOKENS, :],
+                out=mixed_of_pass[g][:, 0:LAST, 0:MM_TOKENS, :],
                 in_=mm_values[:, :, 0 : LAST * MM_TOKENS].rearrange("p t (s n) -> p s n t", s=LAST),
             )
             nc.scalar.copy(
@@ -206,38 +205,36 @@ def tile_moe_pa_k_kernel(tc, encodings, domain_encs, Us, out):
         def quantise_pass(g):
             if not is_pass(g):
                 return
-            u_codes = work.tile([P, SOURCES * RANK], U32, align_bytes=64)
-            u_scales = work.tile([P, SOURCES * RANK], U8, align_bytes=64)
-            nc.vector.quantize_mx(
-                out=u_codes[:].bitcast(FP8X4),
-                scales=u_scales[:],
-                in_=u_grouped_of_pass[g][:].rearrange("p s r t -> p (s r t)"),
-            )
-            diff_codes = work.tile([P, SOURCES, TOKENS], U32, align_bytes=64)
-            diff_scales = work.tile([P, SOURCES, TOKENS], U8, align_bytes=64)
-            for values, lo, hi in (
-                (diff_of_pass[g][:, 0:2].rearrange("p s n t -> p (s n t)"), 0, 2),
-                (diff_last_of_pass[g][:].rearrange("p n t -> p (n t)"), LAST, SOURCES),
-                (diff_of_pass[g][:, 2].rearrange("p n t -> p (n t)"), 2, LAST),
-            ):
+            codes = work.tile([P, SOURCES, TOKENS], U32, align_bytes=64)
+            scales = work.tile([P, SOURCES, TOKENS], U8, align_bytes=64)
+            codes_last = work.tile([P, 1, TOKENS], U32, align_bytes=64)
+            scales_last = work.tile([P, 1, TOKENS], U8, align_bytes=64)
+
+            def quantise(values, code_words, scale_bytes):
                 nc.vector.quantize_mx(
-                    out=diff_codes[:, lo:hi, :].rearrange("p s n -> p (s n)").bitcast(FP8X4),
-                    scales=diff_scales[:, lo:hi, :].rearrange("p s n -> p (s n)"),
-                    in_=values,
+                    out=code_words.rearrange("p s n -> p (s n)").bitcast(FP8X4),
+                    scales=scale_bytes.rearrange("p s n -> p (s n)"),
+                    in_=values.rearrange("p s n t -> p (s n t)"),
                 )
-            codes_of_pass[g] = (u_codes, u_scales, diff_codes, diff_scales)
+
+            mixed = mixed_of_pass[g]
+            quantise(mixed[:, 2:4], codes[:, 2:4], scales[:, 2:4])
+            quantise(diff_last_of_pass[g][:].unsqueeze(1), codes_last[:], scales_last[:])
+            for lo, hi in ((0, 2),) if g < PASSES - 1 else ((0, 1), (1, 2)):
+                quantise(mixed[:, lo:hi], codes[:, lo:hi], scales[:, lo:hi])
+            codes_of_pass[g] = (codes, scales, codes_last, scales_last)
 
         def multiply_pass(g):
             if not is_pass(g):
                 return
-            u_codes, u_scales, diff_codes, diff_scales = codes_of_pass[g]
-            for s in (0, 1, 3, 2):
+            codes, scales, codes_last, scales_last = codes_of_pass[g]
+            for s in SOURCE_ORDER:
                 nc.tensor.matmul_mx(
                     out=acc[s][:],
-                    lhsT=u_codes[:, s * RANK : (s + 1) * RANK].bitcast(FP8X4),
-                    lhsT_scale=u_scales[:, s * RANK : (s + 1) * RANK],
-                    rhs=diff_codes[:, s, :].bitcast(FP8X4),
-                    rhs_scale=diff_scales[:, s, :],
+                    lhsT=codes[:, US_SLOT, s * RANK : (s + 1) * RANK].bitcast(FP8X4),
+                    lhsT_scale=scales[:, US_SLOT, s * RANK : (s + 1) * RANK],
+                    rhs=(codes[:, s, :] if s < LAST else codes_last[:, 0, :]).bitcast(FP8X4),
+                    rhs_scale=scales[:, s, :] if s < LAST else scales_last[:, 0, :],
                     start=(g == 0),
                     stop=(g == PASSES - 1),
                 )
@@ -298,22 +295,30 @@ def tile_moe_pa_k_kernel(tc, encodings, domain_encs, Us, out):
             transpose_half(step - TRANSPOSE_LAG, 0)
             matmul_pass(step - MATMUL_LAG)
             subtract_pass(step - SUBTRACT_LAG)
-            planes_pass(step - SCALAR_LAG)
+            planes_pass(step - PLANES_LAG)
             transpose_half(step - TRANSPOSE_LAG, 1)
-            regroup_pass(step - SCALAR_LAG)
+            regroup_pass(step - REGROUP_LAG)
             quantise_pass(step - MULTIPLY_LAG)
             multiply_pass(step - MULTIPLY_LAG)
 
         dist2 = const.tile([P, SOURCES, TOKEN_BLOCKS], F32)
-        for s in range(SOURCES):
+        for s in SOURCE_ORDER:
             squares = const.tile([P, TOKENS], F32, name="squares%d" % s)
-            nc.scalar.activation(out=squares[:], in_=acc[s][:], func=ACT.Square)
-            turned = bank_pool.tile([P, BANK_WORDS], F32, tag="bank")
-            for b in range(TOKEN_BLOCKS):
-                nc.tensor.transpose(turned[:, b * P : (b + 1) * P], squares[:, b * P : (b + 1) * P], ident[:])
-            nc.vector.tensor_reduce(
-                out=dist2[:, s, :], in_=turned[:].rearrange("p (b r) -> p b r", r=RANK), axis=AXIS.X, op=ALU.add
-            )
+            pieces = 2 if s == SOURCE_ORDER[-1] else 1
+            blocks = TOKEN_BLOCKS // pieces
+            for b_lo in range(0, TOKEN_BLOCKS, blocks):
+                columns = slice(b_lo * P, (b_lo + blocks) * P)
+                nc.scalar.activation(out=squares[:, columns], in_=acc[s][:, columns], func=ACT.Square)
+                turned = bank_pool.tile([P, BANK_WORDS], F32, tag="bank")
+                for b in range(blocks):
+                    lo = (b_lo + b) * P
+                    nc.tensor.transpose(turned[:, b * P : (b + 1) * P], squares[:, lo : lo + P], ident[:])
+                nc.vector.tensor_reduce(
+                    out=dist2[:, s, b_lo : b_lo + blocks],
+                    in_=turned[:, 0 : blocks * P].rearrange("p (b r) -> p b r", r=RANK),
+                    axis=AXIS.X,
+                    op=ALU.add,
+                )
 
         dist = const.tile([P, SOURCES, TOKEN_BLOCKS], F32)
         nc.scalar.activation(out=dist[:], in_=dist2[:], func=ACT.Sqrt)

@@ -16,6 +16,7 @@ P = 128
 PACK = 4
 K_PASS = P * PACK
 SOURCE_ORDER = (2, 3, 0, 1)
+END_ORDER = (2, 0, 1, 3)
 US_SLOT = 3
 PAIR = 2
 
@@ -39,9 +40,8 @@ PLANES_LAG = 3
 INTERLEAVE_LAG = 4
 MULTIPLY_LAG = 4
 
-MM_TOKENS = 46
-MM_TOKENS_LAST = 64
-MM_COLS = LAST * MM_TOKENS + MM_TOKENS_LAST
+MM_TOKENS = 64
+MM_COLS = LAST * MM_TOKENS
 MM_ROWS = 64
 MM_TILES = MATMUL_LAG + 1
 
@@ -133,6 +133,9 @@ def tile_moe_pa_k_kernel(tc, encodings, domain_encs, Us, out):
             if not is_pass(g):
                 return
             diff = mixed_of_pass[g]
+            if g == 0:
+                diff_last = work.tile([P, TOKENS, PACK], BF16, align_bytes=64, bufs=1, tag="diff_last")
+                diff_last_of_pass[g] = diff_last
             for half in range(BANKS_PER_PASS):
                 skip = MM_TOKENS if half == 0 else 0
                 shape = [P, LAST, BANK_TOKENS - skip, PACK]
@@ -142,17 +145,23 @@ def tile_moe_pa_k_kernel(tc, encodings, domain_encs, Us, out):
                     in1=d_cols[:, 0:LAST, g, :].unsqueeze(2).to_broadcast(shape),
                     op=ALU.subtract,
                 )
+                if g == 0:
+                    nc.vector.tensor_tensor(
+                        out=diff_last_of_pass[g][:, half * BANK_TOKENS : (half + 1) * BANK_TOKENS, :],
+                        in0=bank_values(banks_of_pass[g][half]),
+                        in1=d_cols[:, LAST, g, :].unsqueeze(1).to_broadcast([P, BANK_TOKENS, PACK]),
+                        op=ALU.subtract,
+                    )
 
         def planes_pass(g):
-            if not is_pass(g):
+            if not is_pass(g) or g == 0:
                 return
             planes = work.tile([P, PACK, TOKENS], BF16, bufs=INTERLEAVE_LAG - PLANES_LAG + 1)
             for half in range(BANKS_PER_PASS):
-                skip = MM_TOKENS_LAST if half == 0 else 0
                 for t in range(PACK):
                     nc.scalar.activation(
-                        out=planes[:, t, half * BANK_TOKENS + skip : (half + 1) * BANK_TOKENS],
-                        in_=bank_values(banks_of_pass[g][half])[:, skip:, t],
+                        out=planes[:, t, half * BANK_TOKENS : (half + 1) * BANK_TOKENS],
+                        in_=bank_values(banks_of_pass[g][half])[:, :, t],
                         func=ACT.Identity,
                         bias=neg_d_last[:, g * PACK + t : g * PACK + t + 1],
                         scale=1.0,
@@ -179,28 +188,35 @@ def tile_moe_pa_k_kernel(tc, encodings, domain_encs, Us, out):
             mm_values = mm_bank_of_pass[g][:, 0 : PACK * MM_COLS].rearrange("p (t c) -> p t c", t=PACK)
             nc.scalar.copy(
                 out=mixed_of_pass[g][:, 0:LAST, 0:MM_TOKENS, :],
-                in_=mm_values[:, :, 0 : LAST * MM_TOKENS].rearrange("p t (s n) -> p s n t", s=LAST),
-            )
-            nc.scalar.copy(
-                out=diff_last_of_pass[g][:, 0:MM_TOKENS_LAST, :],
-                in_=mm_values[:, :, LAST * MM_TOKENS : MM_COLS].rearrange("p t n -> p n t"),
+                in_=mm_values.rearrange("p t (s n) -> p s n t", s=LAST),
             )
 
         def interleave_last(g):
             if not is_pass(g):
                 return
-            diff_last = work.tile(
-                [P, TOKENS, PACK], BF16, align_bytes=64, bufs=1
-            )
-            nc.gpsimd.tensor_scalar(
-                out=diff_last[:, MM_TOKENS_LAST:, :],
-                in0=planes_of_pass[g][:, :, MM_TOKENS_LAST:].rearrange("p t n -> p n t"),
-                scalar1=1.0,
-                scalar2=0.0,
-                op0=ALU.mult,
-                op1=ALU.add,
-            )
+            if g == 0:
+                return
+            diff_last = work.tile([P, TOKENS, PACK], BF16, align_bytes=64, bufs=1, tag="diff_last")
+            if g < PASSES - 1:
+                nc.gpsimd.tensor_scalar(
+                    out=diff_last[:],
+                    in0=planes_of_pass[g][:].rearrange("p t n -> p n t"),
+                    scalar1=1.0,
+                    scalar2=0.0,
+                    op0=ALU.mult,
+                    op1=ALU.add,
+                )
             diff_last_of_pass[g] = diff_last
+
+        def interleave_very_last(g):
+            if g != PASSES - 1:
+                return
+            for b in range(TOKEN_BLOCKS):
+                tokens = slice(b * P, (b + 1) * P)
+                nc.scalar.copy(
+                    out=diff_last_of_pass[g][:, tokens, :].rearrange("p (c i) t -> p c t i", i=4),
+                    in_=planes_of_pass[g][:, :, tokens].rearrange("p t (c i) -> p c t i", i=4),
+                )
 
         def quantise_pass(g):
             if not is_pass(g):
@@ -219,16 +235,18 @@ def tile_moe_pa_k_kernel(tc, encodings, domain_encs, Us, out):
 
             mixed = mixed_of_pass[g]
             quantise(mixed[:, 2:4], codes[:, 2:4], scales[:, 2:4])
-            quantise(diff_last_of_pass[g][:].unsqueeze(1), codes_last[:], scales_last[:])
-            for lo, hi in ((0, 2),) if g < PASSES - 1 else ((0, 1), (1, 2)):
-                quantise(mixed[:, lo:hi], codes[:, lo:hi], scales[:, lo:hi])
+            if g < PASSES - 1:
+                quantise(diff_last_of_pass[g][:].unsqueeze(1), codes_last[:], scales_last[:])
+            quantise(mixed[:, 0:2], codes[:, 0:2], scales[:, 0:2])
+            if g == PASSES - 1:
+                quantise(diff_last_of_pass[g][:].unsqueeze(1), codes_last[:], scales_last[:])
             codes_of_pass[g] = (codes, scales, codes_last, scales_last)
 
         def multiply_pass(g):
             if not is_pass(g):
                 return
             codes, scales, codes_last, scales_last = codes_of_pass[g]
-            for s in SOURCE_ORDER:
+            for s in SOURCE_ORDER if g < PASSES - 1 else END_ORDER:
                 nc.tensor.matmul_mx(
                     out=acc[s][:],
                     lhsT=codes[:, US_SLOT, s * RANK : (s + 1) * RANK].bitcast(FP8X4),
@@ -256,15 +274,9 @@ def tile_moe_pa_k_kernel(tc, encodings, domain_encs, Us, out):
 
         pick = const.tile([P, MM_COLS], BF16)
         nc.vector.tensor_tensor(
-            out=pick[:, 0 : LAST * MM_TOKENS].rearrange("p (s n) -> p s n", s=LAST),
+            out=pick[:].rearrange("p (s n) -> p s n", s=LAST),
             in0=ident[:, 0:MM_TOKENS].unsqueeze(1).to_broadcast([P, LAST, MM_TOKENS]),
             in1=ident[:, MM_ROWS : MM_ROWS + LAST].unsqueeze(2).to_broadcast([P, LAST, MM_TOKENS]),
-            op=ALU.subtract,
-        )
-        nc.vector.tensor_tensor(
-            out=pick[:, LAST * MM_TOKENS : MM_COLS],
-            in0=ident[:, 0:MM_TOKENS_LAST],
-            in1=ident[:, MM_ROWS + LAST : MM_ROWS + SOURCES].to_broadcast([P, MM_TOKENS_LAST]),
             op=ALU.subtract,
         )
 
@@ -292,6 +304,7 @@ def tile_moe_pa_k_kernel(tc, encodings, domain_encs, Us, out):
             load(step)
             interleave_last(step - INTERLEAVE_LAG)
             copy_share(step - INTERLEAVE_LAG)
+            interleave_very_last(step - INTERLEAVE_LAG)
             transpose_half(step - TRANSPOSE_LAG, 0)
             matmul_pass(step - MATMUL_LAG)
             subtract_pass(step - SUBTRACT_LAG)
@@ -302,9 +315,9 @@ def tile_moe_pa_k_kernel(tc, encodings, domain_encs, Us, out):
             multiply_pass(step - MULTIPLY_LAG)
 
         dist2 = const.tile([P, SOURCES, TOKEN_BLOCKS], F32)
-        for s in SOURCE_ORDER:
+        for s in END_ORDER:
             squares = const.tile([P, TOKENS], F32, name="squares%d" % s)
-            pieces = 2 if s == SOURCE_ORDER[-1] else 1
+            pieces = 2 if s == END_ORDER[-1] else 1
             blocks = TOKEN_BLOCKS // pieces
             for b_lo in range(0, TOKEN_BLOCKS, blocks):
                 columns = slice(b_lo * P, (b_lo + blocks) * P)

@@ -40,9 +40,10 @@ PLANES_LAG = 3
 INTERLEAVE_LAG = 4
 MULTIPLY_LAG = 4
 
-MM_TOKENS = 64
+MM_TOKENS = 68
 MM_COLS = LAST * MM_TOKENS
 MM_ROWS = 64
+MM_REST = MM_TOKENS - MM_ROWS
 MM_TILES = MATMUL_LAG + 1
 
 FLOPS = 2 * SOURCES * TOKENS * HIDDEN * RANK
@@ -77,12 +78,13 @@ def tile_moe_pa_k_kernel(tc, encodings, domain_encs, Us, out):
             x_of_pass[g] = []
             for half in range(BANKS_PER_PASS):
                 x_sb = work.tile([P, BLOCKS_PER_BANK, K_PASS], BF16, bufs=BANKS_PER_PASS * (TRANSPOSE_LAG + 1))
-                nc.sync.dma_start(
-                    out=x_sb[:],
-                    in_=encodings[half * BANK_TOKENS : (half + 1) * BANK_TOKENS, k_lo : k_lo + K_PASS].rearrange(
-                        "(b n) k -> n b k", n=P
-                    ),
-                )
+                step = 1 if g == 0 and half == 0 else BLOCKS_PER_BANK
+                for b in range(0, BLOCKS_PER_BANK, step):
+                    lo = half * BANK_TOKENS + b * P
+                    nc.sync.dma_start(
+                        out=x_sb[:, b : b + step, :],
+                        in_=encodings[lo : lo + step * P, k_lo : k_lo + K_PASS].rearrange("(b n) k -> n b k", n=P),
+                    )
                 x_of_pass[g].append(x_sb)
             u_raw = work.tile([P, SOURCES, PACK * RANK], BF16, bufs=REGROUP_LAG + 2)
             nc.sync.dma_start(
@@ -97,7 +99,9 @@ def tile_moe_pa_k_kernel(tc, encodings, domain_encs, Us, out):
             k_hi = k_lo + K_PASS
             rows = mm_rows[g % MM_TILES]
             nc.sync.dma_start(out=rows[0:MM_ROWS, :], in_=encodings[0:MM_ROWS, k_lo:k_hi])
-            nc.sync.dma_start(out=rows[MM_ROWS : MM_ROWS + SOURCES, :], in_=domain_encs[:, k_lo:k_hi])
+            rest = MM_ROWS + SOURCES
+            nc.sync.dma_start(out=rows[MM_ROWS:rest, :], in_=domain_encs[:, k_lo:k_hi])
+            nc.sync.dma_start(out=rows[rest : rest + MM_REST, :], in_=encodings[MM_ROWS:MM_TOKENS, k_lo:k_hi])
 
         def matmul_pass(g):
             if not is_pass(g):
@@ -237,8 +241,10 @@ def tile_moe_pa_k_kernel(tc, encodings, domain_encs, Us, out):
             quantise(mixed[:, 2:4], codes[:, 2:4], scales[:, 2:4])
             if g < PASSES - 1:
                 quantise(diff_last_of_pass[g][:].unsqueeze(1), codes_last[:], scales_last[:])
-            quantise(mixed[:, 0:2], codes[:, 0:2], scales[:, 0:2])
-            if g == PASSES - 1:
+                quantise(mixed[:, 0:2], codes[:, 0:2], scales[:, 0:2])
+            else:
+                for s in range(2):
+                    quantise(mixed[:, s : s + 1], codes[:, s : s + 1], scales[:, s : s + 1])
                 quantise(diff_last_of_pass[g][:].unsqueeze(1), codes_last[:], scales_last[:])
             codes_of_pass[g] = (codes, scales, codes_last, scales_last)
 
@@ -273,12 +279,13 @@ def tile_moe_pa_k_kernel(tc, encodings, domain_encs, Us, out):
         nc.scalar.activation(out=warm[:], in_=warm[:], func=ACT.Sqrt)
 
         pick = const.tile([P, MM_COLS], BF16)
-        nc.vector.tensor_tensor(
-            out=pick[:].rearrange("p (s n) -> p s n", s=LAST),
-            in0=ident[:, 0:MM_TOKENS].unsqueeze(1).to_broadcast([P, LAST, MM_TOKENS]),
-            in1=ident[:, MM_ROWS : MM_ROWS + LAST].unsqueeze(2).to_broadcast([P, LAST, MM_TOKENS]),
-            op=ALU.subtract,
-        )
+        for lo, count, row in ((0, MM_ROWS, 0), (MM_ROWS, MM_REST, MM_ROWS + SOURCES)):
+            nc.vector.tensor_tensor(
+                out=pick[:].rearrange("p (s n) -> p s n", s=LAST)[:, :, lo : lo + count],
+                in0=ident[:, row : row + count].unsqueeze(1).to_broadcast([P, LAST, count]),
+                in1=ident[:, MM_ROWS : MM_ROWS + LAST].unsqueeze(2).to_broadcast([P, LAST, count]),
+                op=ALU.subtract,
+            )
 
         d_words = d_rows[:].bitcast(F32).rearrange("r (w u) -> r u w", u=PAIR)
         d_bank = bank_pool.tile([P, BANK_WORDS], F32, tag="bank")
@@ -303,13 +310,13 @@ def tile_moe_pa_k_kernel(tc, encodings, domain_encs, Us, out):
         for step in range(PASSES + MULTIPLY_LAG):
             load(step)
             interleave_last(step - INTERLEAVE_LAG)
-            copy_share(step - INTERLEAVE_LAG)
             interleave_very_last(step - INTERLEAVE_LAG)
             transpose_half(step - TRANSPOSE_LAG, 0)
             matmul_pass(step - MATMUL_LAG)
             subtract_pass(step - SUBTRACT_LAG)
             planes_pass(step - PLANES_LAG)
             transpose_half(step - TRANSPOSE_LAG, 1)
+            copy_share(step - MATMUL_LAG)
             regroup_pass(step - REGROUP_LAG)
             quantise_pass(step - MULTIPLY_LAG)
             multiply_pass(step - MULTIPLY_LAG)

from contextlib import ExitStack

import concourse.mybir as mybir
from concourse.masks import make_identity

F32 = mybir.dt.float32
BF16 = mybir.dt.bfloat16
U32 = mybir.dt.uint32
U8 = mybir.dt.uint8
FP8X4 = mybir.dt.float8_e4m3fn_x4
ACT = mybir.ActivationFunctionType
ALU = mybir.AluOpType
AXIS = mybir.AxisListType

P = 128
PACK = 4
K_PASS = P * PACK
SOURCE_ORDER = (2, 3, 0, 1)
END_ORDER = (2, 0, 1, 3)
US_SLOT = 3
PAIR = 2

TOKENS = 512
HIDDEN = 16384
SOURCES = 4
LAST = SOURCES - 1
RANK = 128
PASSES = HIDDEN // K_PASS
TOKEN_BLOCKS = TOKENS // P
BANK_WORDS = 512
BANK_TOKENS = BANK_WORDS // PAIR
BANKS_PER_PASS = TOKENS // BANK_TOKENS
BLOCKS_PER_BANK = BANK_TOKENS // P

TRANSPOSE_LAG = 2
REGROUP_LAG = 2
MATMUL_LAG = 3
SUBTRACT_LAG = 3
PLANES_LAG = 3
INTERLEAVE_LAG = 4
MULTIPLY_LAG = 4

MM_TOKENS = 68
MM_COLS = LAST * MM_TOKENS
MM_ROWS = 64
MM_REST = MM_TOKENS - MM_ROWS
MM_TILES = MATMUL_LAG + 1

FLOPS = 2 * SOURCES * TOKENS * HIDDEN * RANK


def tile_moe_pa_k_kernel(tc, encodings, domain_encs, Us, out):
    nc = tc.nc
    with ExitStack() as ctx:
        const = ctx.enter_context(tc.tile_pool(name="const", bufs=1))
        work = ctx.enter_context(tc.tile_pool(name="work", bufs=2))
        acc_pool = ctx.enter_context(tc.psum_pool(name="acc", bufs=1))
        bank_pool = ctx.enter_context(tc.psum_pool(name="banks", bufs=3))
        mm_pool = ctx.enter_context(tc.psum_pool(name="mm", bufs=1))
        ctx.enter_context(tc.manual_schedule())

        x_of_pass = {}
        u_of_pass = {}
        banks_of_pass = {}
        planes_of_pass = {}
        mixed_of_pass = {}
        diff_last_of_pass = {}
        codes_of_pass = {}
        mm_bank_of_pass = {}

        def is_pass(g):
            return 0 <= g < PASSES

        def load(g):
            if not is_pass(g):
                return
            k_lo = g * K_PASS
            x_of_pass[g] = []
            for half in range(BANKS_PER_PASS):
                x_sb = work.tile([P, BLOCKS_PER_BANK, K_PASS], BF16, bufs=BANKS_PER_PASS * (TRANSPOSE_LAG + 1))
                step = 1 if g == 0 and half == 0 else BLOCKS_PER_BANK
                for b in range(0, BLOCKS_PER_BANK, step):
                    lo = half * BANK_TOKENS + b * P
                    nc.sync.dma_start(
                        out=x_sb[:, b : b + step, :],
                        in_=encodings[lo : lo + step * P, k_lo : k_lo + K_PASS].rearrange("(b n) k -> n b k", n=P),
                    )
                x_of_pass[g].append(x_sb)
            u_raw = work.tile([P, SOURCES, PACK * RANK], BF16, bufs=REGROUP_LAG + 2)
            nc.sync.dma_start(
                out=u_raw[:],
                in_=Us[:, k_lo : k_lo + K_PASS, :].rearrange("s (p t) r -> p s (t r)", t=PACK),
            )
            u_of_pass[g] = u_raw
            load_rows(g)

        def load_rows(g):
            k_lo = g * K_PASS
            k_hi = k_lo + K_PASS
            rows = mm_rows[g % MM_TILES]
            nc.sync.dma_start(out=rows[0:MM_ROWS, :], in_=encodings[0:MM_ROWS, k_lo:k_hi])
            rest = MM_ROWS + SOURCES
            nc.sync.dma_start(out=rows[MM_ROWS:rest, :], in_=domain_encs[:, k_lo:k_hi])
            nc.sync.dma_start(out=rows[rest : rest + MM_REST, :], in_=encodings[MM_ROWS:MM_TOKENS, k_lo:k_hi])

        def matmul_pass(g):
            if not is_pass(g):
                return
            mm_bank = mm_pool.tile([P, 2 * BANK_WORDS], BF16)
            values = mm_bank[:, 0 : PACK * MM_COLS].rearrange("p (t c) -> p t c", t=PACK)
            rows = mm_rows[g % MM_TILES][:].rearrange("n (m t) -> n t m", t=PACK)
            for t in range(PACK):
                nc.tensor.matmul(
                    values[:, t, :],
                    lhsT=rows[:, t, :],
                    rhs=pick[:],
                    start=True,
                    stop=True,
                )
            mm_bank_of_pass[g] = mm_bank

        def transpose_half(g, half):
            if not is_pass(g):
                return
            bank = bank_pool.tile([P, BANK_WORDS], F32, tag="bank")
            bank_words = bank[:].rearrange("p (n u) -> p u n", u=PAIR)
            for b in range(BLOCKS_PER_BANK):
                x_words = x_of_pass[g][half][:, b, :].bitcast(F32).rearrange("n (w u) -> n u w", u=PAIR)
                for u in range(PAIR):
                    nc.tensor.transpose(bank_words[:, u, b * P : (b + 1) * P], x_words[:, u, :], ident[:])
            banks_of_pass.setdefault(g, []).append(bank)

        def bank_values(bank):
            return bank[:].bitcast(BF16).rearrange("p (n t) -> p n t", t=PACK)

        def subtract_pass(g):
            if not is_pass(g):
                return
            diff = mixed_of_pass[g]
            if g == 0:
                diff_last = work.tile([P, TOKENS, PACK], BF16, align_bytes=64, bufs=1, tag="diff_last")
                diff_last_of_pass[g] = diff_last
            for half in range(BANKS_PER_PASS):
                skip = MM_TOKENS if half == 0 else 0
                shape = [P, LAST, BANK_TOKENS - skip, PACK]
                nc.vector.tensor_tensor(
                    out=diff[:, 0:LAST, half * BANK_TOKENS + skip : (half + 1) * BANK_TOKENS, :],
                    in0=bank_values(banks_of_pass[g][half])[:, skip:, :].unsqueeze(1).to_broadcast(shape),
                    in1=d_cols[:, 0:LAST, g, :].unsqueeze(2).to_broadcast(shape),
                    op=ALU.subtract,
                )
                if g == 0:
                    nc.vector.tensor_tensor(
                        out=diff_last_of_pass[g][:, half * BANK_TOKENS : (half + 1) * BANK_TOKENS, :],
                        in0=bank_values(banks_of_pass[g][half]),
                        in1=d_cols[:, LAST, g, :].unsqueeze(1).to_broadcast([P, BANK_TOKENS, PACK]),
                        op=ALU.subtract,
                    )

        def planes_pass(g):
            if not is_pass(g) or g == 0:
                return
            planes = work.tile([P, PACK, TOKENS], BF16, bufs=INTERLEAVE_LAG - PLANES_LAG + 1)
            for half in range(BANKS_PER_PASS):
                for t in range(PACK):
                    nc.scalar.activation(
                        out=planes[:, t, half * BANK_TOKENS : (half + 1) * BANK_TOKENS],
                        in_=bank_values(banks_of_pass[g][half])[:, :, t],
                        func=ACT.Identity,
                        bias=neg_d_last[:, g * PACK + t : g * PACK + t + 1],
                        scale=1.0,
                    )
            planes_of_pass[g] = planes

        def regroup_pass(g):
            if not is_pass(g):
                return
            mixed = work.tile(
                [P, SOURCES, TOKENS, PACK], BF16, align_bytes=64, bufs=MULTIPLY_LAG - REGROUP_LAG + 1
            )
            u_grouped = mixed[:, US_SLOT].rearrange("p (s r) t -> p s r t", s=SOURCES)
            for s in range(SOURCES):
                nc.scalar.copy(
                    out=u_grouped[:, s].rearrange("p (c i) t -> p c t i", i=4),
                    in_=u_of_pass[g][:, s].rearrange("p (t c i) -> p c t i", t=PACK, i=4),
                )
            mixed_of_pass[g] = mixed

        def copy_share(g):
            if not is_pass(g):
                return
            mm_values = mm_bank_of_pass[g][:, 0 : PACK * MM_COLS].rearrange("p (t c) -> p t c", t=PACK)
            nc.scalar.copy(
                out=mixed_of_pass[g][:, 0:LAST, 0:MM_TOKENS, :],
                in_=mm_values.rearrange("p t (s n) -> p s n t", s=LAST),
            )

        def interleave_last(g):
            if not is_pass(g):
                return
            if g == 0:
                return
            diff_last = work.tile([P, TOKENS, PACK], BF16, align_bytes=64, bufs=1, tag="diff_last")
            if g < PASSES - 1:
                nc.gpsimd.tensor_scalar(
                    out=diff_last[:],
                    in0=planes_of_pass[g][:].rearrange("p t n -> p n t"),
                    scalar1=1.0,
                    scalar2=0.0,
                    op0=ALU.mult,
                    op1=ALU.add,
                )
            diff_last_of_pass[g] = diff_last

        def interleave_very_last(g):
            if g != PASSES - 1:
                return
            for b in range(TOKEN_BLOCKS):
                tokens = slice(b * P, (b + 1) * P)
                nc.scalar.copy(
                    out=diff_last_of_pass[g][:, tokens, :].rearrange("p (c i) t -> p c t i", i=4),
                    in_=planes_of_pass[g][:, :, tokens].rearrange("p t (c i) -> p c t i", i=4),
                )

        def quantise_pass(g):
            if not is_pass(g):
                return
            codes = work.tile([P, SOURCES, TOKENS], U32, align_bytes=64)
            scales = work.tile([P, SOURCES, TOKENS], U8, align_bytes=64)
            codes_last = work.tile([P, 1, TOKENS], U32, align_bytes=64)
            scales_last = work.tile([P, 1, TOKENS], U8, align_bytes=64)

            def quantise(values, code_words, scale_bytes):
                nc.vector.quantize_mx(
                    out=code_words.rearrange("p s n -> p (s n)").bitcast(FP8X4),
                    scales=scale_bytes.rearrange("p s n -> p (s n)"),
                    in_=values.rearrange("p s n t -> p (s n t)"),
                )

            mixed = mixed_of_pass[g]
            quantise(mixed[:, 2:4], codes[:, 2:4], scales[:, 2:4])
            if g < PASSES - 1:
                quantise(diff_last_of_pass[g][:].unsqueeze(1), codes_last[:], scales_last[:])
                quantise(mixed[:, 0:2], codes[:, 0:2], scales[:, 0:2])
            else:
                for s in range(2):
                    quantise(mixed[:, s : s + 1], codes[:, s : s + 1], scales[:, s : s + 1])
                quantise(diff_last_of_pass[g][:].unsqueeze(1), codes_last[:], scales_last[:])
            codes_of_pass[g] = (codes, scales, codes_last, scales_last)

        def multiply_pass(g):
            if not is_pass(g):
                return
            codes, scales, codes_last, scales_last = codes_of_pass[g]
            for s in SOURCE_ORDER if g < PASSES - 1 else END_ORDER:
                nc.tensor.matmul_mx(
                    out=acc[s][:],
                    lhsT=codes[:, US_SLOT, s * RANK : (s + 1) * RANK].bitcast(FP8X4),
                    lhsT_scale=scales[:, US_SLOT, s * RANK : (s + 1) * RANK],
                    rhs=(codes[:, s, :] if s < LAST else codes_last[:, 0, :]).bitcast(FP8X4),
                    rhs_scale=scales[:, s, :] if s < LAST else scales_last[:, 0, :],
                    start=(g == 0),
                    stop=(g == PASSES - 1),
                )

        d_rows = const.tile([P, K_PASS], BF16)
        nc.sync.dma_start(out=d_rows[:], in_=domain_encs.rearrange("s (g k) -> (s g) k", k=K_PASS))

        mm_rows = [const.tile([P, K_PASS], BF16, name="mm_rows%d" % i) for i in range(MM_TILES)]
        for rows in mm_rows:
            nc.vector.memset(rows[MM_ROWS:P, :], 0.0)

        ident = const.tile([P, P], F32)
        make_identity(nc, ident[:])
        alphas = const.tile([P, P], F32)
        nc.vector.memset(alphas[:], 0.0)
        warm = const.tile([P, 1], F32)
        nc.vector.memset(warm[:], 1.0)
        nc.scalar.activation(out=warm[:], in_=warm[:], func=ACT.Sqrt)

        pick = const.tile([P, MM_COLS], BF16)
        for lo, count, row in ((0, MM_ROWS, 0), (MM_ROWS, MM_REST, MM_ROWS + SOURCES)):
            nc.vector.tensor_tensor(
                out=pick[:].rearrange("p (s n) -> p s n", s=LAST)[:, :, lo : lo + count],
                in0=ident[:, row : row + count].unsqueeze(1).to_broadcast([P, LAST, count]),
                in1=ident[:, MM_ROWS : MM_ROWS + LAST].unsqueeze(2).to_broadcast([P, LAST, count]),
                op=ALU.subtract,
            )

        d_words = d_rows[:].bitcast(F32).rearrange("r (w u) -> r u w", u=PAIR)
        d_bank = bank_pool.tile([P, BANK_WORDS], F32, tag="bank")
        for u in range(PAIR):
            nc.tensor.transpose(d_bank[:, u * P : (u + 1) * P], d_words[:, u, :], ident[:])
        d_cols = const.tile([P, SOURCES, PASSES, PACK], BF16)
        nc.vector.tensor_copy(
            out=d_cols[:].rearrange("p s g t -> p (s g t)").bitcast(F32).rearrange("p (r u) -> p r u", u=PAIR),
            in_=d_bank[:, 0 : PAIR * P].rearrange("p (u r) -> p r u", u=PAIR),
        )
        neg_d_last = const.tile([P, PASSES * PACK], F32)
        nc.vector.tensor_scalar(
            out=neg_d_last[:],
            in0=d_cols[:, LAST].rearrange("p g t -> p (g t)"),
            scalar1=-1.0,
            scalar2=None,
            op0=ALU.mult,
        )

        acc = [acc_pool.tile([P, TOKENS], F32, name="acc%d" % s) for s in range(SOURCES)]

        for step in range(PASSES + MULTIPLY_LAG):
            load(step)
            interleave_last(step - INTERLEAVE_LAG)
            interleave_very_last(step - INTERLEAVE_LAG)
            transpose_half(step - TRANSPOSE_LAG, 0)
            matmul_pass(step - MATMUL_LAG)
            subtract_pass(step - SUBTRACT_LAG)
            planes_pass(step - PLANES_LAG)
            transpose_half(step - TRANSPOSE_LAG, 1)
            copy_share(step - MATMUL_LAG)
            regroup_pass(step - REGROUP_LAG)
            quantise_pass(step - MULTIPLY_LAG)
            multiply_pass(step - MULTIPLY_LAG)

        dist2 = const.tile([P, SOURCES, TOKEN_BLOCKS], F32)
        for s in END_ORDER:
            squares = const.tile([P, TOKENS], F32, name="squares%d" % s)
            pieces = 2 if s == END_ORDER[-1] else 1
            blocks = TOKEN_BLOCKS // pieces
            for b_lo in range(0, TOKEN_BLOCKS, blocks):
                columns = slice(b_lo * P, (b_lo + blocks) * P)
                nc.scalar.activation(out=squares[:, columns], in_=acc[s][:, columns], func=ACT.Square)
                turned = bank_pool.tile([P, BANK_WORDS], F32, tag="bank")
                for b in range(blocks):
                    lo = (b_lo + b) * P
                    nc.tensor.transpose(turned[:, b * P : (b + 1) * P], squares[:, lo : lo + P], ident[:])
                nc.vector.tensor_reduce(
                    out=dist2[:, s, b_lo : b_lo + blocks],
                    in_=turned[:, 0 : blocks * P].rearrange("p (b r) -> p b r", r=RANK),
                    axis=AXIS.X,
                    op=ALU.add,
                )

        dist = const.tile([P, SOURCES, TOKEN_BLOCKS], F32)
        nc.scalar.activation(out=dist[:], in_=dist2[:], func=ACT.Sqrt)
        nc.scalar.activation(out=warm[:], in_=warm[:], func=ACT.Exp)
        nearest = const.tile([P, TOKEN_BLOCKS], F32)
        nc.vector.tensor_reduce(out=nearest[:], in_=dist[:].rearrange("p s b -> p b s"), axis=AXIS.X, op=ALU.min)
        excess = const.tile([P, SOURCES, TOKEN_BLOCKS], F32)
        nc.vector.tensor_tensor(
            out=excess[:],
            in0=dist[:],
            in1=nearest[:].unsqueeze(1).to_broadcast([P, SOURCES, TOKEN_BLOCKS]),
            op=ALU.subtract,
        )
        weights = const.tile([P, SOURCES, TOKEN_BLOCKS], F32)
        nc.scalar.activation(out=weights[:], in_=excess[:], func=ACT.Exp, scale=-1.0)
        total = const.tile([P, TOKEN_BLOCKS], F32)
        nc.vector.tensor_reduce(out=total[:], in_=weights[:].rearrange("p s b -> p b s"), axis=AXIS.X, op=ALU.add)
        inv_total = const.tile([P, TOKEN_BLOCKS], F32)
        nc.vector.reciprocal(out=inv_total[:], in_=total[:])
        n_rows = SOURCES * TOKEN_BLOCKS
        nc.vector.tensor_tensor(
            out=alphas[:, 0:n_rows].rearrange("p (s b) -> p s b", s=SOURCES),
            in0=weights[:],
            in1=inv_total[:].unsqueeze(1).to_broadcast([P, SOURCES, TOKEN_BLOCKS]),
            op=ALU.mult,
        )
        alphas_bank = bank_pool.tile([P, BANK_WORDS], F32, tag="bank")
        nc.tensor.transpose(alphas_bank[:, 0:P], alphas[:], ident[:])
        alphas_rows = const.tile([P, P], F32)
        nc.vector.tensor_copy(out=alphas_rows[:], in_=alphas_bank[:, 0:P])
        nc.sync.dma_start(out=out.rearrange("s (b n) -> (s b) n", n=P), in_=alphas_rows[0:n_rows, :])
